import numpy as np
import ml_dtypes


def mxq(x, axis, fmt="e4m3"):
    dtype, down = {"e4m3": (ml_dtypes.float8_e4m3fn, 7), "e5m2": (ml_dtypes.float8_e5m2, 14)}[fmt]
    v = np.moveaxis(np.asarray(x, np.float32).astype(ml_dtypes.bfloat16).astype(np.float64), axis, -1)
    blocks = v.reshape(v.shape[:-1] + (-1, 32))
    amax = np.abs(blocks).max(-1, keepdims=True)
    byte = np.maximum(np.where(amax > 0, np.frexp(amax)[1] - 1 + 127, 0) - down, 1)
    scale = np.exp2(byte - 127.0)
    codes = (blocks / scale).astype(np.float32).astype(dtype).astype(np.float64)
    return np.moveaxis((codes * scale).reshape(v.shape), -1, axis)


WIDE = False


def mx_kscale(k):
    if not WIDE:
        return np.ones(k)
    levels = np.array([20, -20, 10, -10, 0])
    a = np.random.permutation(np.resize(levels, k // 512 * 4)).reshape(k // 512, 4)
    idx = np.arange(k)
    return np.exp2(a[idx // 512, idx % 128 // 32])


BF16 = ml_dtypes.bfloat16


def bf(x):
    return np.asarray(x, np.float32).astype(BF16)


def f64(x):
    return np.asarray(x).astype(np.float64)


B, A, C, P = 256, 3, 1024, 1024
N = A * A + 1
T = B * N


def scramble(y):
    return y.transpose(0, 2, 1).reshape(B, N, C)


def unscramble(z):
    return z.reshape(B, C, N).transpose(0, 2, 1)


def setup_inputs():
    s = mx_kscale(T).reshape(B, N, 1)
    z = np.random.standard_normal((B, N, C)) * 1.6 / np.sqrt(N) * s
    w = np.random.standard_normal((P, C)) * 2.0 / np.sqrt(C)
    b = np.random.standard_normal(P) * 0.1
    g = np.random.standard_normal((B, N, P)) * np.exp2(np.random.randint(-12, 1, (B, N, 1))) / s
    return {"y_attn": bf(np.ascontiguousarray(unscramble(z))),
            "w_proj": bf(w),
            "b_proj": bf(b),
            "grad_out": bf(g)}


def reference(y_attn, w_proj, b_proj, grad_out):
    z = scramble(f64(y_attn)).reshape(T, C)
    g = f64(grad_out).reshape(T, P)
    return mxq(g, 0, "e5m2").T @ mxq(z, 0, "e4m3")

@@ -1,0 +1,171 @@
+from contextlib import ExitStack
+
+import concourse.mybir as mybir
+
+FLOPS = 2 * 2560 * 1024 * 1024
+BYTES = 2 * 2560 * 1024 * 2 + 1024 * 1024 * 4
+
+BF16 = mybir.dt.bfloat16
+F32 = mybir.dt.float32
+U32 = mybir.dt.uint32
+U8 = mybir.dt.uint8
+E4M3_X4 = mybir.dt.float8_e4m3fn_x4
+E5M2_X4 = mybir.dt.float8_e5m2_x4
+
+P = 128
+PACK = 4
+TOKENS = 10
+CHANNELS = 1024
+FEATURES = 1024
+BLOCK_ROWS = 32
+BLOCK_PARTS = BLOCK_ROWS // PACK
+GROUP_IMAGES = 16
+GROUP_ROWS = GROUP_IMAGES * TOKENS
+GROUPS = P // BLOCK_PARTS
+PASSES = GROUP_ROWS // BLOCK_ROWS
+
+WORD_ELEMS = PACK * CHANNELS
+LEAD = 2
+RUN = (LEAD + WORD_ELEMS + TOKENS - 1) // TOKENS
+WINDOW = RUN * TOKENS
+PAD = 3
+ROW_PITCH = 416
+SBUF_BLOCK = 16
+
+M_TILE = 128
+N_TILE = 512
+HALF = FEATURES // 2
+M_TILES_PER_HALF = HALF // M_TILE
+N_TILES = CHANNELS // N_TILE
+
+
+def load_z_rows(nc, y_groups, z_rows, blk):
+    for w in range(BLOCK_PARTS):
+        window_start = WORD_ELEMS * (BLOCK_PARTS * blk + w) - LEAD
+        first_channel, first_token = divmod(window_start, TOKENS)
+        turn = TOKENS - first_token
+        for row_lo, row_hi, carry in ((0, turn, 0), (turn, TOKENS, 1)):
+            if row_lo == row_hi:
+                continue
+            token_lo = first_token + row_lo - TOKENS * carry
+            token_hi = token_lo + row_hi - row_lo
+            place = 1 if row_hi <= LEAD else 0
+            last_place = RUN - 2 if row_lo >= TOKENS - LEAD else RUN - 1
+            while place <= last_place:
+                image, channel = divmod(first_channel + carry + place, CHANNELS)
+                count = min(last_place - place + 1, CHANNELS - channel)
+                nc.sync.dma_start(
+                    out=z_rows[w:P:BLOCK_PARTS, blk, row_lo:row_hi, PAD + place : PAD + place + count],
+                    in_=y_groups[:, image, token_lo:token_hi, channel : channel + count],
+                )
+                place += count
+
+
+def regroup(engine_copy, grouped, planes):
+    engine_copy(
+        out=grouped.rearrange("p (c i) t -> p c t i", i=4),
+        in_=planes.rearrange("p t (c i) -> p c t i", i=4),
+    )
+
+
+def tile_attention_pa_kernel(tc, y_attn, w_proj, b_proj, grad_out, out):
+    nc = tc.nc
+    y_groups = y_attn.rearrange("(grp img) tok c -> grp img tok c", img=GROUP_IMAGES)
+    g_groups = grad_out.rearrange("(grp img) i c -> grp (img i) c", img=GROUP_IMAGES)
+
+    with ExitStack() as ctx:
+        keep = ctx.enter_context(tc.tile_pool(name="keep", bufs=1))
+        stage = ctx.enter_context(tc.tile_pool(name="stage", bufs=2))
+        result = ctx.enter_context(tc.tile_pool(name="result", bufs=4))
+        psum = ctx.enter_context(tc.psum_pool(name="psum", bufs=8))
+
+        z_rows = keep.tile([P, PASSES, TOKENS, ROW_PITCH], BF16)
+        g_planes = keep.tile([P, PASSES, 2, PACK, HALF], BF16)
+        z_codes = keep.tile([P, PASSES, CHANNELS], U32, align_bytes=64)
+        z_scales = keep.tile([P, PASSES, CHANNELS], U8, align_bytes=64)
+        g_codes = keep.tile([P, PASSES, FEATURES], U32, align_bytes=64)
+        g_scales = keep.tile([P, PASSES, FEATURES], U8, align_bytes=64)
+
+        nc.vector.memset(z_rows[:, :, 0:LEAD, 0:SBUF_BLOCK], 0.0)
+        nc.vector.memset(z_rows[:, :, TOKENS - LEAD : TOKENS, ROW_PITCH - SBUF_BLOCK : ROW_PITCH], 0.0)
+
+        def load_g(blk, half):
+            nc.sync.dma_start(
+                out=g_planes[:, blk, half],
+                in_=g_groups[:, BLOCK_ROWS * blk : BLOCK_ROWS * (blk + 1), HALF * half : HALF * (half + 1)],
+            )
+
+        def quantise_g(engine_copy, blk, half):
+            g_grouped = stage.tile([P, HALF, PACK], BF16, align_bytes=64)
+            regroup(engine_copy, g_grouped[:], g_planes[:, blk, half])
+            cols = slice(HALF * half, HALF * (half + 1))
+            nc.vector.quantize_mx(
+                out=g_codes[:, blk, cols].bitcast(E5M2_X4),
+                scales=g_scales[:, blk, cols],
+                in_=g_grouped[:].rearrange("p c t -> p (c t)"),
+            )
+
+        def quantise_z(blk):
+            z_stream = stage.tile([P, WINDOW], BF16)
+            nc.vector.tensor_copy(
+                out=z_stream[:].rearrange("p (q r) -> p q r", r=TOKENS),
+                in_=z_rows[:, blk, :, PAD : PAD + RUN].rearrange("p r q -> p q r"),
+            )
+            z_grouped = stage.tile([P, CHANNELS, PACK], BF16, align_bytes=64)
+            regroup(
+                nc.scalar.copy,
+                z_grouped[:],
+                z_stream[:, LEAD : LEAD + WORD_ELEMS].rearrange("p (t c) -> p t c", t=PACK),
+            )
+            nc.vector.quantize_mx(
+                out=z_codes[:, blk, :].bitcast(E4M3_X4),
+                scales=z_scales[:, blk, :],
+                in_=z_grouped[:].rearrange("p c t -> p (c t)"),
+            )
+
+        def mx_pass(acc, blk, m, n):
+            m_cols = slice(M_TILE * m, M_TILE * (m + 1))
+            n_cols = slice(N_TILE * n, N_TILE * (n + 1))
+            nc.tensor.matmul_mx(
+                out=acc[:],
+                lhsT=g_codes[:, blk, m_cols].bitcast(E5M2_X4),
+                lhsT_scale=g_scales[:, blk, m_cols],
+                rhs=z_codes[:, blk, n_cols].bitcast(E4M3_X4),
+                rhs_scale=z_scales[:, blk, n_cols],
+                start=(blk == 0),
+                stop=(blk == PASSES - 1),
+            )
+
+        def store_rows(m, accs):
+            rows = result.tile([P, CHANNELS], F32)
+            nc.vector.tensor_copy(out=rows[:, 0:N_TILE], in_=accs[0][:])
+            nc.scalar.copy(out=rows[:, N_TILE : 2 * N_TILE], in_=accs[1][:])
+            nc.sync.dma_start(out=out[M_TILE * m : M_TILE * (m + 1), :], in_=rows[:])
+
+        for blk in range(PASSES):
+            load_z_rows(nc, y_groups, z_rows, blk)
+            load_g(blk, 0)
+        for blk in range(PASSES):
+            load_g(blk, 1)
+
+        accs = [
+            [psum.tile([P, N_TILE], F32, name="acc_%d_%d" % (m, n), tag="acc") for n in range(N_TILES)]
+            for m in range(M_TILES_PER_HALF)
+        ]
+        for blk in range(PASSES):
+            quantise_z(blk)
+            quantise_g(nc.scalar.copy, blk, 0)
+            for m in range(M_TILES_PER_HALF):
+                for n in range(N_TILES):
+                    mx_pass(accs[m][n], blk, m, n)
+        for blk in range(PASSES):
+            quantise_g(nc.vector.tensor_copy, blk, 1)
+        for m in range(M_TILES_PER_HALF):
+            store_rows(m, accs[m])
+
+        for m in range(M_TILES_PER_HALF, 2 * M_TILES_PER_HALF):
+            accs_m = [psum.tile([P, N_TILE], F32, name="acc_%d_%d" % (m, n), tag="acc") for n in range(N_TILES)]
+            for n in range(N_TILES):
+                for blk in range(PASSES):
+                    mx_pass(accs_m[n], blk, m, n)
+            store_rows(m, accs_m)

@@ -108,8 +108,8 @@ def tile_attention_pa_kernel(tc, y_attn, w_proj, b_proj, grad_out, out):
         def quantise_z(blk):
             z_stream = stage.tile([P, WINDOW], BF16)
             nc.vector.tensor_copy(
-                out=z_stream[:].rearrange("p (q r) -> p q r", r=TOKENS),
-                in_=z_rows[:, blk, :, PAD : PAD + RUN].rearrange("p r q -> p q r"),
+                out=z_stream[:].rearrange("p (q i r) -> p q r i", i=2, r=TOKENS),
+                in_=z_rows[:, blk, :, PAD : PAD + RUN].rearrange("p r (q i) -> p q r i", i=2),
             )
             z_grouped = stage.tile([P, CHANNELS, PACK], BF16, align_bytes=64)
             regroup(

@@ -83,8 +83,10 @@ def tile_attention_pa_kernel(tc, y_attn, w_proj, b_proj, grad_out, out):
         g_planes = keep.tile([P, PASSES, 2, PACK, HALF], BF16)
         z_codes = keep.tile([P, PASSES, CHANNELS], U32, align_bytes=64)
         z_scales = keep.tile([P, PASSES, CHANNELS], U8, align_bytes=64)
-        g_codes = keep.tile([P, PASSES, FEATURES], U32, align_bytes=64)
-        g_scales = keep.tile([P, PASSES, FEATURES], U8, align_bytes=64)
+        gl_codes = keep.tile([P, PASSES, HALF], U32, align_bytes=64)
+        gl_scales = keep.tile([P, PASSES, HALF], U8, align_bytes=64)
+        gr_codes = keep.tile([P, M_TILES_PER_HALF, PASSES, M_TILE], U32, align_bytes=64)
+        gr_scales = keep.tile([P, M_TILES_PER_HALF, PASSES, M_TILE], U8, align_bytes=64)
 
         nc.vector.memset(z_rows[:, :, 0:LEAD, 0:SBUF_BLOCK], 0.0)
         nc.vector.memset(z_rows[:, :, TOKENS - LEAD : TOKENS, ROW_PITCH - SBUF_BLOCK : ROW_PITCH], 0.0)
@@ -95,28 +97,52 @@ def tile_attention_pa_kernel(tc, y_attn, w_proj, b_proj, grad_out, out):
                 in_=g_groups[:, BLOCK_ROWS * blk : BLOCK_ROWS * (blk + 1), HALF * half : HALF * (half + 1)],
             )
 
-        def quantise_g(engine_copy, blk, half):
-            g_grouped = stage.tile([P, HALF, PACK], BF16, align_bytes=64)
-            regroup(engine_copy, g_grouped[:], g_planes[:, blk, half])
-            cols = slice(HALF * half, HALF * (half + 1))
+        def regroup_g_left(blk):
+            gl_grouped = stage.tile([P, HALF, PACK], BF16, align_bytes=64)
+            regroup(nc.scalar.copy, gl_grouped[:], g_planes[:, blk, 0])
+            return gl_grouped
+
+        def quantise_g_left(gl_grouped, blk):
             nc.vector.quantize_mx(
-                out=g_codes[:, blk, cols].bitcast(E5M2_X4),
-                scales=g_scales[:, blk, cols],
-                in_=g_grouped[:].rearrange("p c t -> p (c t)"),
+                out=gl_codes[:, blk, :].bitcast(E5M2_X4),
+                scales=gl_scales[:, blk, :],
+                in_=gl_grouped[:].rearrange("p c t -> p (c t)"),
             )
 
-        def quantise_z(blk):
+        def regroup_g_right(k):
+            gr_grouped = stage.tile([P, PASSES, M_TILE, PACK], BF16, align_bytes=64)
+            nc.vector.tensor_copy(
+                out=gr_grouped[:].rearrange("p b (c i) t -> p b c t i", i=4),
+                in_=g_planes[:, :, 1, :, M_TILE * k : M_TILE * (k + 1)].rearrange("p b t (c i) -> p b c t i", i=4),
+            )
+            return gr_grouped
+
+        def quantise_g_right(gr_grouped, k):
+            for lo, hi in ((0, PASSES - 1), (PASSES - 1, PASSES)):
+                nc.vector.quantize_mx(
+                    out=gr_codes[:, k, lo:hi, :].rearrange("p b c -> p (b c)").bitcast(E5M2_X4),
+                    scales=gr_scales[:, k, lo:hi, :].rearrange("p b c -> p (b c)"),
+                    in_=gr_grouped[:, lo:hi].rearrange("p b c t -> p (b c t)"),
+                )
+
+        def weave_z(blk):
             z_stream = stage.tile([P, WINDOW], BF16)
             nc.vector.tensor_copy(
-                out=z_stream[:].rearrange("p (q i r) -> p q r i", i=2, r=TOKENS),
-                in_=z_rows[:, blk, :, PAD : PAD + RUN].rearrange("p r (q i) -> p q r i", i=2),
+                out=z_stream[:].rearrange("p (q r) -> p q r", r=TOKENS),
+                in_=z_rows[:, blk, :, PAD : PAD + RUN].rearrange("p r q -> p q r"),
             )
+            return z_stream
+
+        def regroup_z(z_stream):
             z_grouped = stage.tile([P, CHANNELS, PACK], BF16, align_bytes=64)
             regroup(
                 nc.scalar.copy,
                 z_grouped[:],
                 z_stream[:, LEAD : LEAD + WORD_ELEMS].rearrange("p (t c) -> p t c", t=PACK),
             )
+            return z_grouped
+
+        def quantise_z(z_grouped, blk):
             nc.vector.quantize_mx(
                 out=z_codes[:, blk, :].bitcast(E4M3_X4),
                 scales=z_scales[:, blk, :],
@@ -124,48 +150,67 @@ def tile_attention_pa_kernel(tc, y_attn, w_proj, b_proj, grad_out, out):
             )
 
         def mx_pass(acc, blk, m, n):
-            m_cols = slice(M_TILE * m, M_TILE * (m + 1))
+            if m < M_TILES_PER_HALF:
+                m_cols = slice(M_TILE * m, M_TILE * (m + 1))
+                g_words, g_plane = gl_codes[:, blk, m_cols], gl_scales[:, blk, m_cols]
+            else:
+                k = m - M_TILES_PER_HALF
+                g_words, g_plane = gr_codes[:, k, blk, :], gr_scales[:, k, blk, :]
             n_cols = slice(N_TILE * n, N_TILE * (n + 1))
             nc.tensor.matmul_mx(
                 out=acc[:],
-                lhsT=g_codes[:, blk, m_cols].bitcast(E5M2_X4),
-                lhsT_scale=g_scales[:, blk, m_cols],
+                lhsT=g_words.bitcast(E5M2_X4),
+                lhsT_scale=g_plane,
                 rhs=z_codes[:, blk, n_cols].bitcast(E4M3_X4),
                 rhs_scale=z_scales[:, blk, n_cols],
                 start=(blk == 0),
                 stop=(blk == PASSES - 1),
             )
 
-        def store_rows(m, accs):
+        def store_rows(m, accs, left_copy):
             rows = result.tile([P, CHANNELS], F32)
-            nc.vector.tensor_copy(out=rows[:, 0:N_TILE], in_=accs[0][:])
+            left_copy(out=rows[:, 0:N_TILE], in_=accs[0][:])
             nc.scalar.copy(out=rows[:, N_TILE : 2 * N_TILE], in_=accs[1][:])
             nc.sync.dma_start(out=out[M_TILE * m : M_TILE * (m + 1), :], in_=rows[:])
 
+        def new_accs(m):
+            return [psum.tile([P, N_TILE], F32, name="acc_%d_%d" % (m, n), tag="acc") for n in range(N_TILES)]
+
+        ctx.enter_context(tc.manual_schedule())
+
         for blk in range(PASSES):
-            load_z_rows(nc, y_groups, z_rows, blk)
             load_g(blk, 0)
+            load_z_rows(nc, y_groups, z_rows, blk)
         for blk in range(PASSES):
             load_g(blk, 1)
 
-        accs = [
-            [psum.tile([P, N_TILE], F32, name="acc_%d_%d" % (m, n), tag="acc") for n in range(N_TILES)]
-            for m in range(M_TILES_PER_HALF)
-        ]
+        accs = [new_accs(m) for m in range(M_TILES_PER_HALF)]
+        z_stream = weave_z(0)
         for blk in range(PASSES):
-            quantise_z(blk)
-            quantise_g(nc.scalar.copy, blk, 0)
+            gl_grouped = regroup_g_left(blk)
+            z_grouped = regroup_z(z_stream)
+            if blk + 1 < PASSES:
+                z_stream = weave_z(blk + 1)
+            quantise_g_left(gl_grouped, blk)
+            quantise_z(z_grouped, blk)
             for m in range(M_TILES_PER_HALF):
                 for n in range(N_TILES):
                     mx_pass(accs[m][n], blk, m, n)
-        for blk in range(PASSES):
-            quantise_g(nc.vector.tensor_copy, blk, 1)
-        for m in range(M_TILES_PER_HALF):
-            store_rows(m, accs[m])
 
-        for m in range(M_TILES_PER_HALF, 2 * M_TILES_PER_HALF):
-            accs_m = [psum.tile([P, N_TILE], F32, name="acc_%d_%d" % (m, n), tag="acc") for n in range(N_TILES)]
+        gr_grouped = regroup_g_right(0)
+        for k in range(M_TILES_PER_HALF):
+            gr_ready = gr_grouped
+            if k + 1 < M_TILES_PER_HALF:
+                gr_grouped = regroup_g_right(k + 1)
+            quantise_g_right(gr_ready, k)
+
+        for m in range(M_TILES_PER_HALF):
+            store_rows(m, accs[m], nc.scalar.copy)
+
+        for k in range(M_TILES_PER_HALF):
+            m = M_TILES_PER_HALF + k
+            accs_m = new_accs(m)
             for n in range(N_TILES):
                 for blk in range(PASSES):
                     mx_pass(accs_m[n], blk, m, n)
-            store_rows(m, accs_m)
+            store_rows(m, accs_m, nc.scalar.copy if 2 * k < M_TILES_PER_HALF else nc.vector.tensor_copy)

@@ -27,10 +27,9 @@ PASSES = GROUP_ROWS // BLOCK_ROWS
 WORD_ELEMS = PACK * CHANNELS
 LEAD = 2
 RUN = (LEAD + WORD_ELEMS + TOKENS - 1) // TOKENS
-WINDOW = RUN * TOKENS
+RUN_COLUMNS = TOKENS * ((CHANNELS + TOKENS - 1) // TOKENS)
 PAD = 3
 ROW_PITCH = 416
-SBUF_BLOCK = 16
 
 M_TILE = 128
 N_TILE = 512
@@ -68,6 +67,32 @@ def regroup(engine_copy, grouped, planes):
     )
 
 
+def unscramble(nc, z_grouped, z_rows, blk):
+    rows = z_rows[:, blk : blk + 2].rearrange("p b r q -> p (b r q)")
+    columns = z_grouped.rearrange("p (u v) t -> p u v t", v=TOKENS)
+    for v in range(0, TOKENS, 2):
+        steps = (CHANNELS - v + TOKENS - 1) // TOKENS
+        at = []
+        for t in range(PACK):
+            place, row = divmod(LEAD + CHANNELS * t + v, TOKENS)
+            at.append(row * ROW_PITCH + PAD + place)
+        if at[0] < at[1] and at[2] < at[3]:
+            copies = ((0, 1), (2, 3))
+        elif at[0] < at[3] and at[1] < at[2]:
+            copies = ((0, 3), (1, 2))
+        else:
+            copies = ((1, 2), (0,), (3,))
+        for ts in copies:
+            first, last = ts[0], ts[-1]
+            apart = max(at[last] - at[first], 2 * ROW_PITCH)
+            runs = rows[:, at[first] : at[first] + len(ts) * apart].rearrange("p (e s) -> p e s", e=len(ts))
+            runs = runs[:, :, 0 : 2 * ROW_PITCH].rearrange("p e (v q) -> p e v q", v=2)
+            nc.vector.tensor_copy(
+                out=columns[:, 0:steps, v : v + 2, first : last + 1 : max(last - first, 1)],
+                in_=runs[:, :, :, 0:steps].rearrange("p e v q -> p q v e"),
+            )
+
+
 def tile_attention_pa_kernel(tc, y_attn, w_proj, b_proj, grad_out, out):
     nc = tc.nc
     y_groups = y_attn.rearrange("(grp img) tok c -> grp img tok c", img=GROUP_IMAGES)
@@ -75,21 +100,17 @@ def tile_attention_pa_kernel(tc, y_attn, w_proj, b_proj, grad_out, out):
 
     with ExitStack() as ctx:
         keep = ctx.enter_context(tc.tile_pool(name="keep", bufs=1))
-        stage = ctx.enter_context(tc.tile_pool(name="stage", bufs=2))
+        z_stage = ctx.enter_context(tc.tile_pool(name="z_stage", bufs=2))
+        g_stage = ctx.enter_context(tc.tile_pool(name="g_stage", bufs=6))
         result = ctx.enter_context(tc.tile_pool(name="result", bufs=4))
         psum = ctx.enter_context(tc.psum_pool(name="psum", bufs=8))
 
-        z_rows = keep.tile([P, PASSES, TOKENS, ROW_PITCH], BF16)
+        z_rows = keep.tile([P, PASSES + 1, TOKENS, ROW_PITCH], BF16)
         g_planes = keep.tile([P, PASSES, 2, PACK, HALF], BF16)
         z_codes = keep.tile([P, PASSES, CHANNELS], U32, align_bytes=64)
         z_scales = keep.tile([P, PASSES, CHANNELS], U8, align_bytes=64)
-        gl_codes = keep.tile([P, PASSES, HALF], U32, align_bytes=64)
-        gl_scales = keep.tile([P, PASSES, HALF], U8, align_bytes=64)
-        gr_codes = keep.tile([P, M_TILES_PER_HALF, PASSES, M_TILE], U32, align_bytes=64)
-        gr_scales = keep.tile([P, M_TILES_PER_HALF, PASSES, M_TILE], U8, align_bytes=64)
-
-        nc.vector.memset(z_rows[:, :, 0:LEAD, 0:SBUF_BLOCK], 0.0)
-        nc.vector.memset(z_rows[:, :, TOKENS - LEAD : TOKENS, ROW_PITCH - SBUF_BLOCK : ROW_PITCH], 0.0)
+        g_codes = keep.tile([P, PASSES, FEATURES], U32, align_bytes=64)
+        g_scales = keep.tile([P, PASSES, FEATURES], U8, align_bytes=64)
 
         def load_g(blk, half):
             nc.sync.dma_start(
@@ -97,79 +118,47 @@ def tile_attention_pa_kernel(tc, y_attn, w_proj, b_proj, grad_out, out):
                 in_=g_groups[:, BLOCK_ROWS * blk : BLOCK_ROWS * (blk + 1), HALF * half : HALF * (half + 1)],
             )
 
-        def regroup_g_left(blk):
-            gl_grouped = stage.tile([P, HALF, PACK], BF16, align_bytes=64)
-            regroup(nc.scalar.copy, gl_grouped[:], g_planes[:, blk, 0])
-            return gl_grouped
+        def regroup_g(blk, half):
+            g_grouped = g_stage.tile([P, HALF, PACK], BF16, align_bytes=64)
+            regroup(nc.scalar.copy, g_grouped[:], g_planes[:, blk, half])
+            return g_grouped
 
-        def quantise_g_left(gl_grouped, blk):
+        def quantise_g(g_grouped, blk, half):
+            cols = slice(HALF * half, HALF * (half + 1))
             nc.vector.quantize_mx(
-                out=gl_codes[:, blk, :].bitcast(E5M2_X4),
-                scales=gl_scales[:, blk, :],
-                in_=gl_grouped[:].rearrange("p c t -> p (c t)"),
+                out=g_codes[:, blk, cols].bitcast(E5M2_X4),
+                scales=g_scales[:, blk, cols],
+                in_=g_grouped[:].rearrange("p c t -> p (c t)"),
             )
 
-        def regroup_g_right(k):
-            gr_grouped = stage.tile([P, PASSES, M_TILE, PACK], BF16, align_bytes=64)
-            nc.vector.tensor_copy(
-                out=gr_grouped[:].rearrange("p b (c i) t -> p b c t i", i=4),
-                in_=g_planes[:, :, 1, :, M_TILE * k : M_TILE * (k + 1)].rearrange("p b t (c i) -> p b c t i", i=4),
-            )
-            return gr_grouped
-
-        def quantise_g_right(gr_grouped, k):
-            for lo, hi in ((0, PASSES - 1), (PASSES - 1, PASSES)):
-                nc.vector.quantize_mx(
-                    out=gr_codes[:, k, lo:hi, :].rearrange("p b c -> p (b c)").bitcast(E5M2_X4),
-                    scales=gr_scales[:, k, lo:hi, :].rearrange("p b c -> p (b c)"),
-                    in_=gr_grouped[:, lo:hi].rearrange("p b c t -> p (b c t)"),
-                )
-
-        def weave_z(blk):
-            z_stream = stage.tile([P, WINDOW], BF16)
-            nc.vector.tensor_copy(
-                out=z_stream[:].rearrange("p (q r) -> p q r", r=TOKENS),
-                in_=z_rows[:, blk, :, PAD : PAD + RUN].rearrange("p r q -> p q r"),
-            )
-            return z_stream
-
-        def regroup_z(z_stream):
-            z_grouped = stage.tile([P, CHANNELS, PACK], BF16, align_bytes=64)
-            regroup(
-                nc.scalar.copy,
-                z_grouped[:],
-                z_stream[:, LEAD : LEAD + WORD_ELEMS].rearrange("p (t c) -> p t c", t=PACK),
-            )
+        def unscramble_z(blk):
+            z_grouped = z_stage.tile([P, RUN_COLUMNS, PACK], BF16, align_bytes=64)
+            unscramble(nc, z_grouped[:], z_rows, blk)
             return z_grouped
 
         def quantise_z(z_grouped, blk):
             nc.vector.quantize_mx(
                 out=z_codes[:, blk, :].bitcast(E4M3_X4),
                 scales=z_scales[:, blk, :],
-                in_=z_grouped[:].rearrange("p c t -> p (c t)"),
+                in_=z_grouped[:, 0:CHANNELS, :].rearrange("p c t -> p (c t)"),
             )
 
         def mx_pass(acc, blk, m, n):
-            if m < M_TILES_PER_HALF:
-                m_cols = slice(M_TILE * m, M_TILE * (m + 1))
-                g_words, g_plane = gl_codes[:, blk, m_cols], gl_scales[:, blk, m_cols]
-            else:
-                k = m - M_TILES_PER_HALF
-                g_words, g_plane = gr_codes[:, k, blk, :], gr_scales[:, k, blk, :]
+            m_cols = slice(M_TILE * m, M_TILE * (m + 1))
             n_cols = slice(N_TILE * n, N_TILE * (n + 1))
             nc.tensor.matmul_mx(
                 out=acc[:],
-                lhsT=g_words.bitcast(E5M2_X4),
-                lhsT_scale=g_plane,
+                lhsT=g_codes[:, blk, m_cols].bitcast(E5M2_X4),
+                lhsT_scale=g_scales[:, blk, m_cols],
                 rhs=z_codes[:, blk, n_cols].bitcast(E4M3_X4),
                 rhs_scale=z_scales[:, blk, n_cols],
                 start=(blk == 0),
                 stop=(blk == PASSES - 1),
             )
 
-        def store_rows(m, accs, left_copy):
+        def store_rows(m, accs):
             rows = result.tile([P, CHANNELS], F32)
-            left_copy(out=rows[:, 0:N_TILE], in_=accs[0][:])
+            nc.vector.tensor_copy(out=rows[:, 0:N_TILE], in_=accs[0][:])
             nc.scalar.copy(out=rows[:, N_TILE : 2 * N_TILE], in_=accs[1][:])
             nc.sync.dma_start(out=out[M_TILE * m : M_TILE * (m + 1), :], in_=rows[:])
 
@@ -179,38 +168,31 @@ def tile_attention_pa_kernel(tc, y_attn, w_proj, b_proj, grad_out, out):
         ctx.enter_context(tc.manual_schedule())
 
         for blk in range(PASSES):
-            load_g(blk, 0)
             load_z_rows(nc, y_groups, z_rows, blk)
+            load_g(blk, 0)
         for blk in range(PASSES):
             load_g(blk, 1)
 
         accs = [new_accs(m) for m in range(M_TILES_PER_HALF)]
-        z_stream = weave_z(0)
         for blk in range(PASSES):
-            gl_grouped = regroup_g_left(blk)
-            z_grouped = regroup_z(z_stream)
-            if blk + 1 < PASSES:
-                z_stream = weave_z(blk + 1)
-            quantise_g_left(gl_grouped, blk)
+            g_grouped = regroup_g(blk, 0)
+            z_grouped = unscramble_z(blk)
+            quantise_g(g_grouped, blk, 0)
             quantise_z(z_grouped, blk)
             for m in range(M_TILES_PER_HALF):
                 for n in range(N_TILES):
                     mx_pass(accs[m][n], blk, m, n)
 
-        gr_grouped = regroup_g_right(0)
-        for k in range(M_TILES_PER_HALF):
-            gr_ready = gr_grouped
-            if k + 1 < M_TILES_PER_HALF:
-                gr_grouped = regroup_g_right(k + 1)
-            quantise_g_right(gr_ready, k)
+        for blk in range(PASSES):
+            g_grouped = regroup_g(blk, 1)
+            quantise_g(g_grouped, blk, 1)
 
         for m in range(M_TILES_PER_HALF):
-            store_rows(m, accs[m], nc.scalar.copy)
+            store_rows(m, accs[m])
 
-        for k in range(M_TILES_PER_HALF):
-            m = M_TILES_PER_HALF + k
+        for m in range(M_TILES_PER_HALF, 2 * M_TILES_PER_HALF):
             accs_m = new_accs(m)
             for n in range(N_TILES):
                 for blk in range(PASSES):
                     mx_pass(accs_m[n], blk, m, n)
-            store_rows(m, accs_m, nc.scalar.copy if 2 * k < M_TILES_PER_HALF else nc.vector.tensor_copy)
+            store_rows(m, accs_m)

@@ -30,16 +30,21 @@ RUN = (LEAD + WORD_ELEMS + TOKENS - 1) // TOKENS
 RUN_COLUMNS = TOKENS * ((CHANNELS + TOKENS - 1) // TOKENS)
 PAD = 3
 ROW_PITCH = 416
+ROWS_ROOM = 13 * ROW_PITCH
 
 M_TILE = 128
 N_TILE = 512
 HALF = FEATURES // 2
 M_TILES_PER_HALF = HALF // M_TILE
 N_TILES = CHANNELS // N_TILE
+LOADS_AHEAD = 2
 
 
 def load_z_rows(nc, y_groups, z_rows, blk):
-    for w in range(BLOCK_PARTS):
+    rows = z_rows[:, 0 : TOKENS * ROW_PITCH].rearrange("p (r q) -> p r q", q=ROW_PITCH)
+    for i in range(BLOCK_PARTS):
+        w = (i % 2) * (BLOCK_PARTS // 2) + i // 2
+        queue = nc.sync if i % 2 == 0 else nc.scalar
         window_start = WORD_ELEMS * (BLOCK_PARTS * blk + w) - LEAD
         first_channel, first_token = divmod(window_start, TOKENS)
         turn = TOKENS - first_token
@@ -53,8 +58,8 @@ def load_z_rows(nc, y_groups, z_rows, blk):
             while place <= last_place:
                 image, channel = divmod(first_channel + carry + place, CHANNELS)
                 count = min(last_place - place + 1, CHANNELS - channel)
-                nc.sync.dma_start(
-                    out=z_rows[w:P:BLOCK_PARTS, blk, row_lo:row_hi, PAD + place : PAD + place + count],
+                queue.dma_start(
+                    out=rows[w:P:BLOCK_PARTS, row_lo:row_hi, PAD + place : PAD + place + count],
                     in_=y_groups[:, image, token_lo:token_hi, channel : channel + count],
                 )
                 place += count
@@ -67,8 +72,7 @@ def regroup(engine_copy, grouped, planes):
     )
 
 
-def unscramble(nc, z_grouped, z_rows, blk):
-    rows = z_rows[:, blk : blk + 2].rearrange("p b r q -> p (b r q)")
+def unscramble(nc, z_grouped, z_rows):
     columns = z_grouped.rearrange("p (u v) t -> p u v t", v=TOKENS)
     for v in range(0, TOKENS, 2):
         steps = (CHANNELS - v + TOKENS - 1) // TOKENS
@@ -85,7 +89,8 @@ def unscramble(nc, z_grouped, z_rows, blk):
         for ts in copies:
             first, last = ts[0], ts[-1]
             apart = max(at[last] - at[first], 2 * ROW_PITCH)
-            runs = rows[:, at[first] : at[first] + len(ts) * apart].rearrange("p (e s) -> p e s", e=len(ts))
+            assert at[first] + len(ts) * apart <= ROWS_ROOM
+            runs = z_rows[:, at[first] : at[first] + len(ts) * apart].rearrange("p (e s) -> p e s", e=len(ts))
             runs = runs[:, :, 0 : 2 * ROW_PITCH].rearrange("p e (v q) -> p e v q", v=2)
             nc.vector.tensor_copy(
                 out=columns[:, 0:steps, v : v + 2, first : last + 1 : max(last - first, 1)],
@@ -105,7 +110,7 @@ def tile_attention_pa_kernel(tc, y_attn, w_proj, b_proj, grad_out, out):
         result = ctx.enter_context(tc.tile_pool(name="result", bufs=4))
         psum = ctx.enter_context(tc.psum_pool(name="psum", bufs=8))
 
-        z_rows = keep.tile([P, PASSES + 1, TOKENS, ROW_PITCH], BF16)
+        z_rows = [keep.tile([P, ROWS_ROOM], BF16, name="z_rows_%d" % blk) for blk in range(PASSES)]
         g_planes = keep.tile([P, PASSES, 2, PACK, HALF], BF16)
         z_codes = keep.tile([P, PASSES, CHANNELS], U32, align_bytes=64)
         z_scales = keep.tile([P, PASSES, CHANNELS], U8, align_bytes=64)
@@ -133,7 +138,7 @@ def tile_attention_pa_kernel(tc, y_attn, w_proj, b_proj, grad_out, out):
 
         def unscramble_z(blk):
             z_grouped = z_stage.tile([P, RUN_COLUMNS, PACK], BF16, align_bytes=64)
-            unscramble(nc, z_grouped[:], z_rows, blk)
+            unscramble(nc, z_grouped[:], z_rows[blk])
             return z_grouped
 
         def quantise_z(z_grouped, blk):
@@ -167,14 +172,19 @@ def tile_attention_pa_kernel(tc, y_attn, w_proj, b_proj, grad_out, out):
 
         ctx.enter_context(tc.manual_schedule())
 
-        for blk in range(PASSES):
-            load_z_rows(nc, y_groups, z_rows, blk)
+        def load_pass(blk):
+            load_z_rows(nc, y_groups, z_rows[blk], blk)
             load_g(blk, 0)
-        for blk in range(PASSES):
-            load_g(blk, 1)
 
         accs = [new_accs(m) for m in range(M_TILES_PER_HALF)]
+        for blk in range(LOADS_AHEAD):
+            load_pass(blk)
         for blk in range(PASSES):
+            if blk + LOADS_AHEAD < PASSES:
+                load_pass(blk + LOADS_AHEAD)
+            if blk + LOADS_AHEAD == PASSES:
+                for later in range(PASSES):
+                    load_g(later, 1)
             g_grouped = regroup_g(blk, 0)
             z_grouped = unscramble_z(blk)
             quantise_g(g_grouped, blk, 0)

@@ -21,13 +21,11 @@ BLOCK_ROWS = 32
 BLOCK_PARTS = BLOCK_ROWS // PACK
 GROUP_IMAGES = 16
 GROUP_ROWS = GROUP_IMAGES * TOKENS
-GROUPS = P // BLOCK_PARTS
 PASSES = GROUP_ROWS // BLOCK_ROWS
 
 WORD_ELEMS = PACK * CHANNELS
 LEAD = 2
 RUN = (LEAD + WORD_ELEMS + TOKENS - 1) // TOKENS
-RUN_COLUMNS = TOKENS * ((CHANNELS + TOKENS - 1) // TOKENS)
 PAD = 3
 ROW_PITCH = 416
 ROWS_ROOM = 13 * ROW_PITCH
@@ -37,14 +35,13 @@ N_TILE = 512
 HALF = FEATURES // 2
 M_TILES_PER_HALF = HALF // M_TILE
 N_TILES = CHANNELS // N_TILE
-LOADS_AHEAD = 2
+STEPS = (CHANNELS + TOKENS - 1) // TOKENS
+STEP_PITCH = 104
 
 
 def load_z_rows(nc, y_groups, z_rows, blk):
     rows = z_rows[:, 0 : TOKENS * ROW_PITCH].rearrange("p (r q) -> p r q", q=ROW_PITCH)
-    for i in range(BLOCK_PARTS):
-        w = (i % 2) * (BLOCK_PARTS // 2) + i // 2
-        queue = nc.sync if i % 2 == 0 else nc.scalar
+    for w in range(BLOCK_PARTS):
         window_start = WORD_ELEMS * (BLOCK_PARTS * blk + w) - LEAD
         first_channel, first_token = divmod(window_start, TOKENS)
         turn = TOKENS - first_token
@@ -58,7 +55,7 @@ def load_z_rows(nc, y_groups, z_rows, blk):
             while place <= last_place:
                 image, channel = divmod(first_channel + carry + place, CHANNELS)
                 count = min(last_place - place + 1, CHANNELS - channel)
-                queue.dma_start(
+                nc.sync.dma_start(
                     out=rows[w:P:BLOCK_PARTS, row_lo:row_hi, PAD + place : PAD + place + count],
                     in_=y_groups[:, image, token_lo:token_hi, channel : channel + count],
                 )
@@ -72,30 +69,37 @@ def regroup(engine_copy, grouped, planes):
     )
 
 
-def unscramble(nc, z_grouped, z_rows):
-    columns = z_grouped.rearrange("p (u v) t -> p u v t", v=TOKENS)
-    for v in range(0, TOKENS, 2):
-        steps = (CHANNELS - v + TOKENS - 1) // TOKENS
-        at = []
-        for t in range(PACK):
-            place, row = divmod(LEAD + CHANNELS * t + v, TOKENS)
-            at.append(row * ROW_PITCH + PAD + place)
-        if at[0] < at[1] and at[2] < at[3]:
-            copies = ((0, 1), (2, 3))
-        elif at[0] < at[3] and at[1] < at[2]:
-            copies = ((0, 3), (1, 2))
-        else:
-            copies = ((1, 2), (0,), (3,))
-        for ts in copies:
-            first, last = ts[0], ts[-1]
-            apart = max(at[last] - at[first], 2 * ROW_PITCH)
-            assert at[first] + len(ts) * apart <= ROWS_ROOM
-            runs = z_rows[:, at[first] : at[first] + len(ts) * apart].rearrange("p (e s) -> p e s", e=len(ts))
-            runs = runs[:, :, 0 : 2 * ROW_PITCH].rearrange("p e (v q) -> p e v q", v=2)
+def pair_up(nc, z_pairs, z_rows):
+    for h in range(PACK // 2):
+        cuts = {0, CHANNELS % TOKENS, TOKENS}
+        for t in (2 * h, 2 * h + 1):
+            cuts.add(-(LEAD + CHANNELS * t) % TOKENS)
+        cuts = sorted(cuts)
+        for v_lo, v_hi in zip(cuts[:-1], cuts[1:]):
+            steps = (CHANNELS - v_lo + TOKENS - 1) // TOKENS
+            at = []
+            for t in (2 * h, 2 * h + 1):
+                place, row = divmod(LEAD + CHANNELS * t + v_lo, TOKENS)
+                at.append(row * ROW_PITCH + PAD + place)
+            apart = abs(at[1] - at[0])
+            assert (v_hi - v_lo) * ROW_PITCH <= apart and min(at) + 2 * apart <= ROWS_ROOM
+            runs = z_rows[:, min(at) : min(at) + 2 * apart].rearrange("p (e s) -> p e s", e=2)
+            if at[1] < at[0]:
+                runs = runs[:, ::-1]
+            runs = runs[:, :, 0 : (v_hi - v_lo) * ROW_PITCH].rearrange("p e (v q) -> p e v q", q=ROW_PITCH)
             nc.vector.tensor_copy(
-                out=columns[:, 0:steps, v : v + 2, first : last + 1 : max(last - first, 1)],
-                in_=runs[:, :, :, 0:steps].rearrange("p e v q -> p q v e"),
+                out=z_pairs[:, h, v_lo:v_hi, 0 : 2 * steps].rearrange("p v (u e) -> p v u e", e=2),
+                in_=runs[:, :, :, 0:steps].rearrange("p e v u -> p v u e"),
             )
+
+
+def weave(nc, z_grouped, z_pairs):
+    pairs = z_pairs.bitcast(F32)
+    columns = z_grouped.bitcast(F32).rearrange("p (u v h) -> p u v h", v=TOKENS, h=PACK // 2)
+    whole = CHANNELS // TOKENS
+    nc.scalar.copy(out=columns[:, 0:whole], in_=pairs[:, :, :, 0:whole].rearrange("p h v u -> p u v h"))
+    rest = CHANNELS % TOKENS
+    nc.scalar.copy(out=columns[:, whole, 0:rest, :], in_=pairs[:, :, 0:rest, whole].rearrange("p h v -> p v h"))
 
 
 def tile_attention_pa_kernel(tc, y_attn, w_proj, b_proj, grad_out, out):
@@ -106,7 +110,7 @@ def tile_attention_pa_kernel(tc, y_attn, w_proj, b_proj, grad_out, out):
     with ExitStack() as ctx:
         keep = ctx.enter_context(tc.tile_pool(name="keep", bufs=1))
         z_stage = ctx.enter_context(tc.tile_pool(name="z_stage", bufs=2))
-        g_stage = ctx.enter_context(tc.tile_pool(name="g_stage", bufs=6))
+        g_stage = ctx.enter_context(tc.tile_pool(name="g_stage", bufs=3))
         result = ctx.enter_context(tc.tile_pool(name="result", bufs=4))
         psum = ctx.enter_context(tc.psum_pool(name="psum", bufs=8))
 
@@ -123,9 +127,9 @@ def tile_attention_pa_kernel(tc, y_attn, w_proj, b_proj, grad_out, out):
                 in_=g_groups[:, BLOCK_ROWS * blk : BLOCK_ROWS * (blk + 1), HALF * half : HALF * (half + 1)],
             )
 
-        def regroup_g(blk, half):
+        def regroup_g(engine_copy, blk, half):
             g_grouped = g_stage.tile([P, HALF, PACK], BF16, align_bytes=64)
-            regroup(nc.scalar.copy, g_grouped[:], g_planes[:, blk, half])
+            regroup(engine_copy, g_grouped[:], g_planes[:, blk, half])
             return g_grouped
 
         def quantise_g(g_grouped, blk, half):
@@ -136,16 +140,21 @@ def tile_attention_pa_kernel(tc, y_attn, w_proj, b_proj, grad_out, out):
                 in_=g_grouped[:].rearrange("p c t -> p (c t)"),
             )
 
-        def unscramble_z(blk):
-            z_grouped = z_stage.tile([P, RUN_COLUMNS, PACK], BF16, align_bytes=64)
-            unscramble(nc, z_grouped[:], z_rows[blk])
+        def pair_up_z(blk):
+            z_pairs = z_stage.tile([P, PACK // 2, TOKENS, 2 * STEP_PITCH], BF16)
+            pair_up(nc, z_pairs, z_rows[blk])
+            return z_pairs
+
+        def weave_z(z_pairs):
+            z_grouped = z_stage.tile([P, STEPS * TOKENS * PACK], BF16, align_bytes=64)
+            weave(nc, z_grouped[:], z_pairs[:])
             return z_grouped
 
         def quantise_z(z_grouped, blk):
             nc.vector.quantize_mx(
                 out=z_codes[:, blk, :].bitcast(E4M3_X4),
                 scales=z_scales[:, blk, :],
-                in_=z_grouped[:, 0:CHANNELS, :].rearrange("p c t -> p (c t)"),
+                in_=z_grouped[:, 0:WORD_ELEMS],
             )
 
         def mx_pass(acc, blk, m, n):
@@ -172,21 +181,21 @@ def tile_attention_pa_kernel(tc, y_attn, w_proj, b_proj, grad_out, out):
 
         ctx.enter_context(tc.manual_schedule())
 
-        def load_pass(blk):
-            load_z_rows(nc, y_groups, z_rows[blk], blk)
+        load_z_rows(nc, y_groups, z_rows[0], 0)
+        for blk in range(PASSES):
+            if blk + 1 < PASSES:
+                load_z_rows(nc, y_groups, z_rows[blk + 1], blk + 1)
             load_g(blk, 0)
+        for blk in range(PASSES):
+            load_g(blk, 1)
 
         accs = [new_accs(m) for m in range(M_TILES_PER_HALF)]
-        for blk in range(LOADS_AHEAD):
-            load_pass(blk)
+        z_pairs = pair_up_z(0)
         for blk in range(PASSES):
-            if blk + LOADS_AHEAD < PASSES:
-                load_pass(blk + LOADS_AHEAD)
-            if blk + LOADS_AHEAD == PASSES:
-                for later in range(PASSES):
-                    load_g(later, 1)
-            g_grouped = regroup_g(blk, 0)
-            z_grouped = unscramble_z(blk)
+            z_grouped = weave_z(z_pairs)
+            g_grouped = regroup_g(nc.vector.tensor_copy, blk, 0)
+            if blk + 1 < PASSES:
+                z_pairs = pair_up_z(blk + 1)
             quantise_g(g_grouped, blk, 0)
             quantise_z(z_grouped, blk)
             for m in range(M_TILES_PER_HALF):
@@ -194,7 +203,7 @@ def tile_attention_pa_kernel(tc, y_attn, w_proj, b_proj, grad_out, out):
                     mx_pass(accs[m][n], blk, m, n)
 
         for blk in range(PASSES):
-            g_grouped = regroup_g(blk, 1)
+            g_grouped = regroup_g(nc.scalar.copy if blk % 2 == 0 else nc.vector.tensor_copy, blk, 1)
             quantise_g(g_grouped, blk, 1)
 
         for m in range(M_TILES_PER_HALF):

@@ -28,6 +28,7 @@ LEAD = 2
 RUN = (LEAD + WORD_ELEMS + TOKENS - 1) // TOKENS
 PAD = 3
 ROW_PITCH = 416
+ROWS_PER_DMA = 4
 ROWS_ROOM = 13 * ROW_PITCH
 
 M_TILE = 128
@@ -49,16 +50,17 @@ def load_z_rows(nc, y_groups, z_rows, blk):
             if row_lo == row_hi:
                 continue
             token_lo = first_token + row_lo - TOKENS * carry
-            token_hi = token_lo + row_hi - row_lo
             place = 1 if row_hi <= LEAD else 0
             last_place = RUN - 2 if row_lo >= TOKENS - LEAD else RUN - 1
             while place <= last_place:
                 image, channel = divmod(first_channel + carry + place, CHANNELS)
                 count = min(last_place - place + 1, CHANNELS - channel)
-                nc.sync.dma_start(
-                    out=rows[w:P:BLOCK_PARTS, row_lo:row_hi, PAD + place : PAD + place + count],
-                    in_=y_groups[:, image, token_lo:token_hi, channel : channel + count],
-                )
+                for skip in range(0, row_hi - row_lo, ROWS_PER_DMA):
+                    some = min(ROWS_PER_DMA, row_hi - row_lo - skip)
+                    nc.sync.dma_start(
+                        out=rows[w:P:BLOCK_PARTS, row_lo + skip : row_lo + skip + some, PAD + place : PAD + place + count],
+                        in_=y_groups[:, image, token_lo + skip : token_lo + skip + some, channel : channel + count],
+                    )
                 place += count
 
 

@@ -21,14 +21,15 @@ BLOCK_ROWS = 32
 BLOCK_PARTS = BLOCK_ROWS // PACK
 GROUP_IMAGES = 16
 GROUP_ROWS = GROUP_IMAGES * TOKENS
+GROUPS = P // BLOCK_PARTS
 PASSES = GROUP_ROWS // BLOCK_ROWS
 
 WORD_ELEMS = PACK * CHANNELS
 LEAD = 2
 RUN = (LEAD + WORD_ELEMS + TOKENS - 1) // TOKENS
+RUN_COLUMNS = TOKENS * ((CHANNELS + TOKENS - 1) // TOKENS)
 PAD = 3
 ROW_PITCH = 416
-ROWS_PER_DMA = 4
 ROWS_ROOM = 13 * ROW_PITCH
 
 M_TILE = 128
@@ -36,13 +37,13 @@ N_TILE = 512
 HALF = FEATURES // 2
 M_TILES_PER_HALF = HALF // M_TILE
 N_TILES = CHANNELS // N_TILE
-STEPS = (CHANNELS + TOKENS - 1) // TOKENS
-STEP_PITCH = 104
 
 
 def load_z_rows(nc, y_groups, z_rows, blk):
     rows = z_rows[:, 0 : TOKENS * ROW_PITCH].rearrange("p (r q) -> p r q", q=ROW_PITCH)
-    for w in range(BLOCK_PARTS):
+    for i in range(BLOCK_PARTS):
+        w = (i % 2) * (BLOCK_PARTS // 2) + i // 2
+        queue = nc.sync if i % 2 == 0 else nc.scalar
         window_start = WORD_ELEMS * (BLOCK_PARTS * blk + w) - LEAD
         first_channel, first_token = divmod(window_start, TOKENS)
         turn = TOKENS - first_token
@@ -50,17 +51,18 @@ def load_z_rows(nc, y_groups, z_rows, blk):
             if row_lo == row_hi:
                 continue
             token_lo = first_token + row_lo - TOKENS * carry
+            token_hi = token_lo + row_hi - row_lo
             place = 1 if row_hi <= LEAD else 0
             last_place = RUN - 2 if row_lo >= TOKENS - LEAD else RUN - 1
+            place -= min(PAD + place, (first_channel + carry + place) % CHANNELS)
+            last_place += min(ROW_PITCH - 1 - PAD - last_place, CHANNELS - 1 - (first_channel + carry + last_place) % CHANNELS)
             while place <= last_place:
                 image, channel = divmod(first_channel + carry + place, CHANNELS)
                 count = min(last_place - place + 1, CHANNELS - channel)
-                for skip in range(0, row_hi - row_lo, ROWS_PER_DMA):
-                    some = min(ROWS_PER_DMA, row_hi - row_lo - skip)
-                    nc.sync.dma_start(
-                        out=rows[w:P:BLOCK_PARTS, row_lo + skip : row_lo + skip + some, PAD + place : PAD + place + count],
-                        in_=y_groups[:, image, token_lo + skip : token_lo + skip + some, channel : channel + count],
-                    )
+                queue.dma_start(
+                    out=rows[w:P:BLOCK_PARTS, row_lo:row_hi, PAD + place : PAD + place + count],
+                    in_=y_groups[:, image, token_lo:token_hi, channel : channel + count],
+                )
                 place += count
 
 
@@ -71,37 +73,30 @@ def regroup(engine_copy, grouped, planes):
     )
 
 
-def pair_up(nc, z_pairs, z_rows):
-    for h in range(PACK // 2):
-        cuts = {0, CHANNELS % TOKENS, TOKENS}
-        for t in (2 * h, 2 * h + 1):
-            cuts.add(-(LEAD + CHANNELS * t) % TOKENS)
-        cuts = sorted(cuts)
-        for v_lo, v_hi in zip(cuts[:-1], cuts[1:]):
-            steps = (CHANNELS - v_lo + TOKENS - 1) // TOKENS
-            at = []
-            for t in (2 * h, 2 * h + 1):
-                place, row = divmod(LEAD + CHANNELS * t + v_lo, TOKENS)
-                at.append(row * ROW_PITCH + PAD + place)
-            apart = abs(at[1] - at[0])
-            assert (v_hi - v_lo) * ROW_PITCH <= apart and min(at) + 2 * apart <= ROWS_ROOM
-            runs = z_rows[:, min(at) : min(at) + 2 * apart].rearrange("p (e s) -> p e s", e=2)
-            if at[1] < at[0]:
-                runs = runs[:, ::-1]
-            runs = runs[:, :, 0 : (v_hi - v_lo) * ROW_PITCH].rearrange("p e (v q) -> p e v q", q=ROW_PITCH)
+def unscramble(nc, z_grouped, z_rows):
+    columns = z_grouped.rearrange("p (u v) t -> p u v t", v=TOKENS)
+    for v in range(0, TOKENS, 2):
+        steps = (CHANNELS - v + TOKENS - 1) // TOKENS
+        at = []
+        for t in range(PACK):
+            place, row = divmod(LEAD + CHANNELS * t + v, TOKENS)
+            at.append(row * ROW_PITCH + PAD + place)
+        if at[0] < at[1] and at[2] < at[3]:
+            copies = ((0, 1), (2, 3))
+        elif at[0] < at[3] and at[1] < at[2]:
+            copies = ((0, 3), (1, 2))
+        else:
+            copies = ((1, 2), (0,), (3,))
+        for ts in copies:
+            first, last = ts[0], ts[-1]
+            apart = max(at[last] - at[first], 2 * ROW_PITCH)
+            assert at[first] + len(ts) * apart <= ROWS_ROOM
+            runs = z_rows[:, at[first] : at[first] + len(ts) * apart].rearrange("p (e s) -> p e s", e=len(ts))
+            runs = runs[:, :, 0 : 2 * ROW_PITCH].rearrange("p e (v q) -> p e v q", v=2)
             nc.vector.tensor_copy(
-                out=z_pairs[:, h, v_lo:v_hi, 0 : 2 * steps].rearrange("p v (u e) -> p v u e", e=2),
-                in_=runs[:, :, :, 0:steps].rearrange("p e v u -> p v u e"),
+                out=columns[:, 0:steps, v : v + 2, first : last + 1 : max(last - first, 1)],
+                in_=runs[:, :, :, 0:steps].rearrange("p e v q -> p q v e"),
             )
-
-
-def weave(nc, z_grouped, z_pairs):
-    pairs = z_pairs.bitcast(F32)
-    columns = z_grouped.bitcast(F32).rearrange("p (u v h) -> p u v h", v=TOKENS, h=PACK // 2)
-    whole = CHANNELS // TOKENS
-    nc.scalar.copy(out=columns[:, 0:whole], in_=pairs[:, :, :, 0:whole].rearrange("p h v u -> p u v h"))
-    rest = CHANNELS % TOKENS
-    nc.scalar.copy(out=columns[:, whole, 0:rest, :], in_=pairs[:, :, 0:rest, whole].rearrange("p h v -> p v h"))
 
 
 def tile_attention_pa_kernel(tc, y_attn, w_proj, b_proj, grad_out, out):
@@ -112,8 +107,8 @@ def tile_attention_pa_kernel(tc, y_attn, w_proj, b_proj, grad_out, out):
     with ExitStack() as ctx:
         keep = ctx.enter_context(tc.tile_pool(name="keep", bufs=1))
         z_stage = ctx.enter_context(tc.tile_pool(name="z_stage", bufs=2))
-        g_stage = ctx.enter_context(tc.tile_pool(name="g_stage", bufs=3))
-        result = ctx.enter_context(tc.tile_pool(name="result", bufs=4))
+        g_stage = ctx.enter_context(tc.tile_pool(name="g_stage", bufs=6))
+        result = ctx.enter_context(tc.tile_pool(name="result", bufs=8))
         psum = ctx.enter_context(tc.psum_pool(name="psum", bufs=8))
 
         z_rows = [keep.tile([P, ROWS_ROOM], BF16, name="z_rows_%d" % blk) for blk in range(PASSES)]
@@ -129,9 +124,9 @@ def tile_attention_pa_kernel(tc, y_attn, w_proj, b_proj, grad_out, out):
                 in_=g_groups[:, BLOCK_ROWS * blk : BLOCK_ROWS * (blk + 1), HALF * half : HALF * (half + 1)],
             )
 
-        def regroup_g(engine_copy, blk, half):
+        def regroup_g(blk, half):
             g_grouped = g_stage.tile([P, HALF, PACK], BF16, align_bytes=64)
-            regroup(engine_copy, g_grouped[:], g_planes[:, blk, half])
+            regroup(nc.scalar.copy, g_grouped[:], g_planes[:, blk, half])
             return g_grouped
 
         def quantise_g(g_grouped, blk, half):
@@ -142,21 +137,16 @@ def tile_attention_pa_kernel(tc, y_attn, w_proj, b_proj, grad_out, out):
                 in_=g_grouped[:].rearrange("p c t -> p (c t)"),
             )
 
-        def pair_up_z(blk):
-            z_pairs = z_stage.tile([P, PACK // 2, TOKENS, 2 * STEP_PITCH], BF16)
-            pair_up(nc, z_pairs, z_rows[blk])
-            return z_pairs
-
-        def weave_z(z_pairs):
-            z_grouped = z_stage.tile([P, STEPS * TOKENS * PACK], BF16, align_bytes=64)
-            weave(nc, z_grouped[:], z_pairs[:])
+        def unscramble_z(blk):
+            z_grouped = z_stage.tile([P, RUN_COLUMNS, PACK], BF16, align_bytes=64)
+            unscramble(nc, z_grouped[:], z_rows[blk])
             return z_grouped
 
         def quantise_z(z_grouped, blk):
             nc.vector.quantize_mx(
                 out=z_codes[:, blk, :].bitcast(E4M3_X4),
                 scales=z_scales[:, blk, :],
-                in_=z_grouped[:, 0:WORD_ELEMS],
+                in_=z_grouped[:, 0:CHANNELS, :].rearrange("p c t -> p (c t)"),
             )
 
         def mx_pass(acc, blk, m, n):
@@ -173,40 +163,45 @@ def tile_attention_pa_kernel(tc, y_attn, w_proj, b_proj, grad_out, out):
             )
 
         def store_rows(m, accs):
-            rows = result.tile([P, CHANNELS], F32)
-            nc.vector.tensor_copy(out=rows[:, 0:N_TILE], in_=accs[0][:])
-            nc.scalar.copy(out=rows[:, N_TILE : 2 * N_TILE], in_=accs[1][:])
-            nc.sync.dma_start(out=out[M_TILE * m : M_TILE * (m + 1), :], in_=rows[:])
+            for n, engine_copy in enumerate((nc.vector.tensor_copy, nc.scalar.copy)):
+                tile_out = result.tile([P, N_TILE], F32)
+                engine_copy(out=tile_out[:], in_=accs[n][:])
+                nc.sync.dma_start(
+                    out=out[M_TILE * m : M_TILE * (m + 1), N_TILE * n : N_TILE * (n + 1)], in_=tile_out[:]
+                )
 
         def new_accs(m):
             return [psum.tile([P, N_TILE], F32, name="acc_%d_%d" % (m, n), tag="acc") for n in range(N_TILES)]
 
         ctx.enter_context(tc.manual_schedule())
 
-        load_z_rows(nc, y_groups, z_rows[0], 0)
-        for blk in range(PASSES):
-            if blk + 1 < PASSES:
-                load_z_rows(nc, y_groups, z_rows[blk + 1], blk + 1)
-            load_g(blk, 0)
-        for blk in range(PASSES):
-            load_g(blk, 1)
-
         accs = [new_accs(m) for m in range(M_TILES_PER_HALF)]
-        z_pairs = pair_up_z(0)
-        for blk in range(PASSES):
-            z_grouped = weave_z(z_pairs)
-            g_grouped = regroup_g(nc.vector.tensor_copy, blk, 0)
-            if blk + 1 < PASSES:
-                z_pairs = pair_up_z(blk + 1)
-            quantise_g(g_grouped, blk, 0)
-            quantise_z(z_grouped, blk)
-            for m in range(M_TILES_PER_HALF):
-                for n in range(N_TILES):
-                    mx_pass(accs[m][n], blk, m, n)
+        g_grouped = [None] * PASSES
+        load_z_rows(nc, y_groups, z_rows[0], 0)
+        load_g(0, 0)
+        load_z_rows(nc, y_groups, z_rows[1], 1)
+        for blk in range(PASSES + 1):
+            if blk < PASSES:
+                g_grouped[blk] = regroup_g(blk, 0)
+                if blk + 1 < PASSES:
+                    load_g(blk + 1, 0)
+                if blk + 2 < PASSES:
+                    load_z_rows(nc, y_groups, z_rows[blk + 2], blk + 2)
+                if blk + 2 == PASSES:
+                    for later in range(PASSES):
+                        load_g(later, 1)
+                z_grouped = unscramble_z(blk)
+            if blk > 0:
+                quantise_g(g_grouped[blk - 1], blk - 1, 0)
+            if blk < PASSES:
+                quantise_z(z_grouped, blk)
+            if blk > 0:
+                for m in range(M_TILES_PER_HALF):
+                    for n in range(N_TILES):
+                        mx_pass(accs[m][n], blk - 1, m, n)
 
         for blk in range(PASSES):
-            g_grouped = regroup_g(nc.scalar.copy if blk % 2 == 0 else nc.vector.tensor_copy, blk, 1)
-            quantise_g(g_grouped, blk, 1)
+            quantise_g(regroup_g(blk, 1), blk, 1)
 
         for m in range(M_TILES_PER_HALF):
             store_rows(m, accs[m])

@@ -39,7 +39,29 @@ M_TILES_PER_HALF = HALF // M_TILE
 N_TILES = CHANNELS // N_TILE
 
 
-def load_z_rows(nc, y_groups, z_rows, blk):
+def load_from_one_before(nc, queue, y_attn, rows, first_pair, w, row_lo, row_hi, at, image, token_lo, channel, count):
+    assert channel == 0
+    y_stream = y_attn.rearrange("b tok c -> (b tok c)")
+    y_flat = y_attn.rearrange("(grp img) tok c -> grp (img tok c)", img=GROUP_IMAGES)
+    skip = 1 if image == 0 and token_lo == 0 else 0
+    rows_left = row_hi - row_lo - skip
+    start = (image * TOKENS + token_lo + skip) * CHANNELS - 1
+    queue.dma_start(
+        out=rows[w:P:BLOCK_PARTS, row_lo + skip : row_hi, at - 1 : at + count],
+        in_=y_flat[:, start : start + rows_left * CHANNELS].rearrange("g (t c) -> g t c", c=CHANNELS)[:, :, 0 : count + 1],
+    )
+    if skip:
+        group_elems = GROUP_IMAGES * TOKENS * CHANNELS
+        later_groups = y_stream[group_elems - 1 : GROUPS * group_elems - 1].rearrange("(g x) -> g x", x=group_elems)
+        queue.dma_start(
+            out=rows[w + BLOCK_PARTS : P : BLOCK_PARTS, row_lo, at - 1 : at + count],
+            in_=later_groups[:, 0 : count + 1],
+        )
+        queue.dma_start(out=rows[w : w + 1, row_lo, at + 1 : at + count], in_=y_attn[0:1, 0, 1:count])
+        queue.dma_start(out=first_pair[0:1, :], in_=y_attn[0:1, 0, 0:2])
+
+
+def load_z_rows(nc, y_attn, y_groups, z_rows, first_pair, blk):
     rows = z_rows[:, 0 : TOKENS * ROW_PITCH].rearrange("p (r q) -> p r q", q=ROW_PITCH)
     for i in range(BLOCK_PARTS):
         w = (i % 2) * (BLOCK_PARTS // 2) + i // 2
@@ -59,10 +81,14 @@ def load_z_rows(nc, y_groups, z_rows, blk):
             while place <= last_place:
                 image, channel = divmod(first_channel + carry + place, CHANNELS)
                 count = min(last_place - place + 1, CHANNELS - channel)
-                queue.dma_start(
-                    out=rows[w:P:BLOCK_PARTS, row_lo:row_hi, PAD + place : PAD + place + count],
-                    in_=y_groups[:, image, token_lo:token_hi, channel : channel + count],
-                )
+                at = PAD + place
+                if at % 2 == 0:
+                    queue.dma_start(
+                        out=rows[w:P:BLOCK_PARTS, row_lo:row_hi, at : at + count],
+                        in_=y_groups[:, image, token_lo:token_hi, channel : channel + count],
+                    )
+                else:
+                    load_from_one_before(nc, queue, y_attn, rows, first_pair, w, row_lo, row_hi, at, image, token_lo, channel, count)
                 place += count
 
 
@@ -112,6 +138,7 @@ def tile_attention_pa_kernel(tc, y_attn, w_proj, b_proj, grad_out, out):
         psum = ctx.enter_context(tc.psum_pool(name="psum", bufs=8))
 
         z_rows = [keep.tile([P, ROWS_ROOM], BF16, name="z_rows_%d" % blk) for blk in range(PASSES)]
+        first_pair = keep.tile([P, 2], BF16)
         g_planes = keep.tile([P, PASSES, 2, PACK, HALF], BF16)
         z_codes = keep.tile([P, PASSES, CHANNELS], U32, align_bytes=64)
         z_scales = keep.tile([P, PASSES, CHANNELS], U8, align_bytes=64)
@@ -177,16 +204,19 @@ def tile_attention_pa_kernel(tc, y_attn, w_proj, b_proj, grad_out, out):
 
         accs = [new_accs(m) for m in range(M_TILES_PER_HALF)]
         g_grouped = [None] * PASSES
-        load_z_rows(nc, y_groups, z_rows[0], 0)
+        load_z_rows(nc, y_attn, y_groups, z_rows[0], first_pair, 0)
+        nc.vector.tensor_copy(
+            out=z_rows[0][0:1, LEAD * ROW_PITCH + PAD : LEAD * ROW_PITCH + PAD + 2], in_=first_pair[0:1, :]
+        )
         load_g(0, 0)
-        load_z_rows(nc, y_groups, z_rows[1], 1)
+        load_z_rows(nc, y_attn, y_groups, z_rows[1], first_pair, 1)
         for blk in range(PASSES + 1):
             if blk < PASSES:
                 g_grouped[blk] = regroup_g(blk, 0)
                 if blk + 1 < PASSES:
                     load_g(blk + 1, 0)
                 if blk + 2 < PASSES:
-                    load_z_rows(nc, y_groups, z_rows[blk + 2], blk + 2)
+                    load_z_rows(nc, y_attn, y_groups, z_rows[blk + 2], first_pair, blk + 2)
                 if blk + 2 == PASSES:
                     for later in range(PASSES):
                         load_g(later, 1)

@@ -30,13 +30,15 @@ RUN = (LEAD + WORD_ELEMS + TOKENS - 1) // TOKENS
 RUN_COLUMNS = TOKENS * ((CHANNELS + TOKENS - 1) // TOKENS)
 PAD = 3
 ROW_PITCH = 416
-ROWS_ROOM = 13 * ROW_PITCH
+ROWS_ROOM = 14 * ROW_PITCH
 
 M_TILE = 128
 N_TILE = 512
 HALF = FEATURES // 2
 M_TILES_PER_HALF = HALF // M_TILE
 N_TILES = CHANNELS // N_TILE
+TENS_PER_BANK = N_TILE // TOKENS
+BANK_MAIN = TOKENS * TENS_PER_BANK
 
 
 def load_from_one_before(nc, queue, y_attn, rows, first_pair, w, row_lo, row_hi, at, image, token_lo, channel, count):
@@ -100,29 +102,51 @@ def regroup(engine_copy, grouped, planes):
 
 
 def unscramble(nc, z_grouped, z_rows):
-    columns = z_grouped.rearrange("p (u v) t -> p u v t", v=TOKENS)
-    for v in range(0, TOKENS, 2):
-        steps = (CHANNELS - v + TOKENS - 1) // TOKENS
-        at = []
-        for t in range(PACK):
-            place, row = divmod(LEAD + CHANNELS * t + v, TOKENS)
-            at.append(row * ROW_PITCH + PAD + place)
-        if at[0] < at[1] and at[2] < at[3]:
-            copies = ((0, 1), (2, 3))
-        elif at[0] < at[3] and at[1] < at[2]:
-            copies = ((0, 3), (1, 2))
-        else:
-            copies = ((1, 2), (0,), (3,))
-        for ts in copies:
-            first, last = ts[0], ts[-1]
-            apart = max(at[last] - at[first], 2 * ROW_PITCH)
-            assert at[first] + len(ts) * apart <= ROWS_ROOM
-            runs = z_rows[:, at[first] : at[first] + len(ts) * apart].rearrange("p (e s) -> p e s", e=len(ts))
-            runs = runs[:, :, 0 : 2 * ROW_PITCH].rearrange("p e (v q) -> p e v q", v=2)
+    banks = z_grouped.rearrange("p (n c) t -> p n c t", n=N_TILES)
+    tens = N_TILES * TENS_PER_BANK
+
+    def start_of(t, v):
+        place, row = divmod(LEAD + CHANNELS * t + v, TOKENS)
+        return row * ROW_PITCH + PAD + place
+
+    for v in range(TOKENS):
+        at = [start_of(t, v) for t in range(PACK)]
+        columns = banks[:, :, TENS_PER_BANK * v : TENS_PER_BANK * (v + 1), :]
+        if at[1] - at[0] == at[3] - at[2]:
+            far, near = at[1] - at[0], at[2] - at[0]
+            assert abs(far) >= 2 * abs(near) and abs(near) >= tens and min(at) + 2 * abs(far) <= ROWS_ROOM
+            runs = z_rows[:, min(at) : min(at) + 2 * abs(far)].rearrange("p (l s) -> p l s", l=2)
+            runs = runs[:, :, 0 : 2 * abs(near)].rearrange("p l (h s) -> p l h s", h=2)
+            if far < 0:
+                runs = runs[:, ::-1]
+            if near < 0:
+                runs = runs[:, :, ::-1]
             nc.vector.tensor_copy(
-                out=columns[:, 0:steps, v : v + 2, first : last + 1 : max(last - first, 1)],
-                in_=runs[:, :, :, 0:steps].rearrange("p e v q -> p q v e"),
+                out=columns.rearrange("p n u (h l) -> p n u h l", h=2),
+                in_=runs[:, :, :, 0:tens].rearrange("p l h (n u) -> p n u h l", n=N_TILES),
             )
+        else:
+            for first, last in ((0, 3), (1, 2)):
+                apart = at[last] - at[first]
+                assert apart >= tens and at[first] + 2 * apart <= ROWS_ROOM
+                runs = z_rows[:, at[first] : at[first] + 2 * apart].rearrange("p (e s) -> p e s", e=2)
+                nc.vector.tensor_copy(
+                    out=columns[:, :, :, first : last + 1 : last - first],
+                    in_=runs[:, :, 0:tens].rearrange("p e (n u) -> p n u e", n=N_TILES),
+                )
+    for h in range(2):
+        first = start_of(2 * h, 0) + tens
+        far = start_of(2 * h + 1, 0) - start_of(2 * h, 0)
+        assert far >= PACK * ROW_PITCH and first + 2 * far <= ROWS_ROOM
+        for y in range(1, 4):
+            assert start_of(2 * h, y) == start_of(2 * h, 0) + y * ROW_PITCH
+            assert start_of(2 * h + 1, y) == start_of(2 * h + 1, 0) + y * ROW_PITCH
+        runs = z_rows[:, first : first + 2 * far].rearrange("p (l s) -> p l s", l=2)
+        runs = runs[:, :, 0 : 4 * ROW_PITCH].rearrange("p l (y q) -> p l y q", y=4)
+        nc.vector.tensor_copy(
+            out=banks[:, :, BANK_MAIN:N_TILE, 2 * h : 2 * h + 2],
+            in_=runs[:, :, :, 0:1].rearrange("p l (n x) o -> p n x (l o)", n=N_TILES),
+        )
 
 
 def tile_attention_pa_kernel(tc, y_attn, w_proj, b_proj, grad_out, out):
@@ -134,7 +158,7 @@ def tile_attention_pa_kernel(tc, y_attn, w_proj, b_proj, grad_out, out):
         keep = ctx.enter_context(tc.tile_pool(name="keep", bufs=1))
         z_stage = ctx.enter_context(tc.tile_pool(name="z_stage", bufs=2))
         g_stage = ctx.enter_context(tc.tile_pool(name="g_stage", bufs=6))
-        result = ctx.enter_context(tc.tile_pool(name="result", bufs=8))
+        result = ctx.enter_context(tc.tile_pool(name="result", bufs=4))
         psum = ctx.enter_context(tc.psum_pool(name="psum", bufs=8))
 
         z_rows = [keep.tile([P, ROWS_ROOM], BF16, name="z_rows_%d" % blk) for blk in range(PASSES)]
@@ -165,7 +189,7 @@ def tile_attention_pa_kernel(tc, y_attn, w_proj, b_proj, grad_out, out):
             )
 
         def unscramble_z(blk):
-            z_grouped = z_stage.tile([P, RUN_COLUMNS, PACK], BF16, align_bytes=64)
+            z_grouped = z_stage.tile([P, CHANNELS, PACK], BF16, align_bytes=64)
             unscramble(nc, z_grouped[:], z_rows[blk])
             return z_grouped
 
@@ -173,7 +197,7 @@ def tile_attention_pa_kernel(tc, y_attn, w_proj, b_proj, grad_out, out):
             nc.vector.quantize_mx(
                 out=z_codes[:, blk, :].bitcast(E4M3_X4),
                 scales=z_scales[:, blk, :],
-                in_=z_grouped[:, 0:CHANNELS, :].rearrange("p c t -> p (c t)"),
+                in_=z_grouped[:].rearrange("p c t -> p (c t)"),
             )
 
         def mx_pass(acc, blk, m, n):
@@ -190,12 +214,18 @@ def tile_attention_pa_kernel(tc, y_attn, w_proj, b_proj, grad_out, out):
             )
 
         def store_rows(m, accs):
+            row_out = result.tile([P, CHANNELS], F32)
             for n, engine_copy in enumerate((nc.vector.tensor_copy, nc.scalar.copy)):
-                tile_out = result.tile([P, N_TILE], F32)
-                engine_copy(out=tile_out[:], in_=accs[n][:])
-                nc.sync.dma_start(
-                    out=out[M_TILE * m : M_TILE * (m + 1), N_TILE * n : N_TILE * (n + 1)], in_=tile_out[:]
+                engine_copy(
+                    out=row_out[:, BANK_MAIN * n : BANK_MAIN * (n + 1)].rearrange("p (u v) -> p u v", v=TOKENS),
+                    in_=accs[n][:, 0:BANK_MAIN].rearrange("p (v u) -> p u v", v=TOKENS),
                 )
+                rest = N_TILE - BANK_MAIN
+                engine_copy(
+                    out=row_out[:, N_TILES * BANK_MAIN + rest * n : N_TILES * BANK_MAIN + rest * (n + 1)],
+                    in_=accs[n][:, BANK_MAIN:N_TILE],
+                )
+            nc.sync.dma_start(out=out[M_TILE * m : M_TILE * (m + 1), :], in_=row_out[:])
 
         def new_accs(m):
             return [psum.tile([P, N_TILE], F32, name="acc_%d_%d" % (m, n), tag="acc") for n in range(N_TILES)]

@@ -67,7 +67,7 @@ def load_z_rows(nc, y_attn, y_groups, z_rows, first_pair, blk):
     rows = z_rows[:, 0 : TOKENS * ROW_PITCH].rearrange("p (r q) -> p r q", q=ROW_PITCH)
     for i in range(BLOCK_PARTS):
         w = (i % 2) * (BLOCK_PARTS // 2) + i // 2
-        queue = nc.sync if i % 2 == 0 else nc.scalar
+        queue = nc.sync
         window_start = WORD_ELEMS * (BLOCK_PARTS * blk + w) - LEAD
         first_channel, first_token = divmod(window_start, TOKENS)
         turn = TOKENS - first_token

@@ -101,7 +101,10 @@ def regroup(engine_copy, grouped, planes):
     )
 
 
-def unscramble(nc, z_grouped, z_rows):
+SCALAR_V = (6, 7)
+
+
+def unscramble(nc, z_grouped, z_rows, on_scalar):
     banks = z_grouped.rearrange("p (n c) t -> p n c t", n=N_TILES)
     tens = N_TILES * TENS_PER_BANK
 
@@ -110,6 +113,9 @@ def unscramble(nc, z_grouped, z_rows):
         return row * ROW_PITCH + PAD + place
 
     for v in range(TOKENS):
+        if (v in SCALAR_V) != on_scalar:
+            continue
+        engine_copy = nc.scalar.copy if on_scalar else nc.vector.tensor_copy
         at = [start_of(t, v) for t in range(PACK)]
         columns = banks[:, :, TENS_PER_BANK * v : TENS_PER_BANK * (v + 1), :]
         if at[1] - at[0] == at[3] - at[2]:
@@ -121,7 +127,7 @@ def unscramble(nc, z_grouped, z_rows):
                 runs = runs[:, ::-1]
             if near < 0:
                 runs = runs[:, :, ::-1]
-            nc.vector.tensor_copy(
+            engine_copy(
                 out=columns.rearrange("p n u (h l) -> p n u h l", h=2),
                 in_=runs[:, :, :, 0:tens].rearrange("p l h (n u) -> p n u h l", n=N_TILES),
             )
@@ -130,11 +136,11 @@ def unscramble(nc, z_grouped, z_rows):
                 apart = at[last] - at[first]
                 assert apart >= tens and at[first] + 2 * apart <= ROWS_ROOM
                 runs = z_rows[:, at[first] : at[first] + 2 * apart].rearrange("p (e s) -> p e s", e=2)
-                nc.vector.tensor_copy(
+                engine_copy(
                     out=columns[:, :, :, first : last + 1 : last - first],
                     in_=runs[:, :, 0:tens].rearrange("p e (n u) -> p n u e", n=N_TILES),
                 )
-    for h in range(2):
+    for h in range(0 if on_scalar else 2):
         first = start_of(2 * h, 0) + tens
         far = start_of(2 * h + 1, 0) - start_of(2 * h, 0)
         assert far >= PACK * ROW_PITCH and first + 2 * far <= ROWS_ROOM
@@ -163,6 +169,7 @@ def tile_attention_pa_kernel(tc, y_attn, w_proj, b_proj, grad_out, out):
 
         z_rows = [keep.tile([P, ROWS_ROOM], BF16, name="z_rows_%d" % blk) for blk in range(PASSES)]
         first_pair = keep.tile([P, 2], BF16)
+        warm = keep.tile([P, 2], F32)
         g_planes = keep.tile([P, PASSES, 2, PACK, HALF], BF16)
         z_codes = keep.tile([P, PASSES, CHANNELS], U32, align_bytes=64)
         z_scales = keep.tile([P, PASSES, CHANNELS], U8, align_bytes=64)
@@ -188,10 +195,8 @@ def tile_attention_pa_kernel(tc, y_attn, w_proj, b_proj, grad_out, out):
                 in_=g_grouped[:].rearrange("p c t -> p (c t)"),
             )
 
-        def unscramble_z(blk):
-            z_grouped = z_stage.tile([P, CHANNELS, PACK], BF16, align_bytes=64)
-            unscramble(nc, z_grouped[:], z_rows[blk])
-            return z_grouped
+        def new_z_grouped():
+            return z_stage.tile([P, CHANNELS, PACK], BF16, align_bytes=64, name="z_grouped")
 
         def quantise_z(z_grouped, blk):
             nc.vector.quantize_mx(
@@ -213,18 +218,22 @@ def tile_attention_pa_kernel(tc, y_attn, w_proj, b_proj, grad_out, out):
                 stop=(blk == PASSES - 1),
             )
 
-        def store_rows(m, accs):
-            row_out = result.tile([P, CHANNELS], F32)
-            for n, engine_copy in enumerate((nc.vector.tensor_copy, nc.scalar.copy)):
-                engine_copy(
-                    out=row_out[:, BANK_MAIN * n : BANK_MAIN * (n + 1)].rearrange("p (u v) -> p u v", v=TOKENS),
-                    in_=accs[n][:, 0:BANK_MAIN].rearrange("p (v u) -> p u v", v=TOKENS),
-                )
-                rest = N_TILE - BANK_MAIN
-                engine_copy(
-                    out=row_out[:, N_TILES * BANK_MAIN + rest * n : N_TILES * BANK_MAIN + rest * (n + 1)],
-                    in_=accs[n][:, BANK_MAIN:N_TILE],
-                )
+        def new_row_out():
+            return result.tile([P, CHANNELS], F32, name="row_out")
+
+        def empty_bank(row_out, acc, n):
+            engine_copy = (nc.vector.tensor_copy, nc.scalar.copy)[n]
+            engine_copy(
+                out=row_out[:, BANK_MAIN * n : BANK_MAIN * (n + 1)].rearrange("p (u v) -> p u v", v=TOKENS),
+                in_=acc[:, 0:BANK_MAIN].rearrange("p (v u) -> p u v", v=TOKENS),
+            )
+            rest = N_TILE - BANK_MAIN
+            engine_copy(
+                out=row_out[:, N_TILES * BANK_MAIN + rest * n : N_TILES * BANK_MAIN + rest * (n + 1)],
+                in_=acc[:, BANK_MAIN:N_TILE],
+            )
+
+        def store_row(m, row_out):
             nc.sync.dma_start(out=out[M_TILE * m : M_TILE * (m + 1), :], in_=row_out[:])
 
         def new_accs(m):
@@ -233,42 +242,55 @@ def tile_attention_pa_kernel(tc, y_attn, w_proj, b_proj, grad_out, out):
         ctx.enter_context(tc.manual_schedule())
 
         accs = [new_accs(m) for m in range(M_TILES_PER_HALF)]
-        g_grouped = [None] * PASSES
+        nc.vector.memset(warm[:, 0:1], 0.0)
+        nc.scalar.copy(out=warm[:, 1:2], in_=warm[:, 0:1])
         load_z_rows(nc, y_attn, y_groups, z_rows[0], first_pair, 0)
         nc.vector.tensor_copy(
             out=z_rows[0][0:1, LEAD * ROW_PITCH + PAD : LEAD * ROW_PITCH + PAD + 2], in_=first_pair[0:1, :]
         )
-        load_g(0, 0)
-        load_z_rows(nc, y_attn, y_groups, z_rows[1], first_pair, 1)
-        for blk in range(PASSES + 1):
-            if blk < PASSES:
-                g_grouped[blk] = regroup_g(blk, 0)
-                if blk + 1 < PASSES:
-                    load_g(blk + 1, 0)
-                if blk + 2 < PASSES:
-                    load_z_rows(nc, y_attn, y_groups, z_rows[blk + 2], first_pair, blk + 2)
-                if blk + 2 == PASSES:
-                    for later in range(PASSES):
-                        load_g(later, 1)
-                z_grouped = unscramble_z(blk)
-            if blk > 0:
-                quantise_g(g_grouped[blk - 1], blk - 1, 0)
-            if blk < PASSES:
-                quantise_z(z_grouped, blk)
-            if blk > 0:
-                for m in range(M_TILES_PER_HALF):
-                    for n in range(N_TILES):
-                        mx_pass(accs[m][n], blk - 1, m, n)
+        for blk in range(PASSES):
+            load_g(blk, 0)
+            if blk + 1 < PASSES:
+                load_z_rows(nc, y_attn, y_groups, z_rows[blk + 1], first_pair, blk + 1)
+        for blk in range(PASSES):
+            load_g(blk, 1)
 
         for blk in range(PASSES):
+            z_grouped = new_z_grouped()
+            unscramble(nc, z_grouped[:], z_rows[blk], True)
+            g_grouped = regroup_g(blk, 0)
+            unscramble(nc, z_grouped[:], z_rows[blk], False)
+            quantise_g(g_grouped, blk, 0)
+            quantise_z(z_grouped, blk)
+            for m in range(M_TILES_PER_HALF):
+                for n in range(N_TILES):
+                    mx_pass(accs[m][n], blk, m, n)
+
+        rows_out = [new_row_out() for m in range(M_TILES_PER_HALF)]
+        for blk in range(PASSES):
             quantise_g(regroup_g(blk, 1), blk, 1)
+            if blk < M_TILES_PER_HALF:
+                for n in range(N_TILES):
+                    empty_bank(rows_out[blk], accs[blk][n], n)
+                store_row(blk, rows_out[blk])
 
-        for m in range(M_TILES_PER_HALF):
-            store_rows(m, accs[m])
-
-        for m in range(M_TILES_PER_HALF, 2 * M_TILES_PER_HALF):
+        first = [new_accs(m) for m in (4, 5)]
+        for blk in range(PASSES):
+            for i in range(2):
+                for n in range(N_TILES):
+                    mx_pass(first[i][n], blk, 4 + i, n)
+        for m in (6, 7):
             accs_m = new_accs(m)
             for n in range(N_TILES):
                 for blk in range(PASSES):
                     mx_pass(accs_m[n], blk, m, n)
-            store_rows(m, accs_m)
+            if m == 6:
+                for i in range(2):
+                    row_out = new_row_out()
+                    for n in range(N_TILES):
+                        empty_bank(row_out, first[i][n], n)
+                    store_row(4 + i, row_out)
+            row_out = new_row_out()
+            for n in range(N_TILES):
+                empty_bank(row_out, accs_m[n], n)
+            store_row(m, row_out)

@@ -104,7 +104,10 @@ def regroup(engine_copy, grouped, planes):
 SCALAR_V = (6, 7)
 
 
-def unscramble(nc, z_grouped, z_rows, on_scalar):
+VECTOR_V = tuple(v for v in range(TOKENS) if v not in SCALAR_V)
+
+
+def unscramble(nc, z_grouped, z_rows, engine_copy, some_v, last_columns):
     banks = z_grouped.rearrange("p (n c) t -> p n c t", n=N_TILES)
     tens = N_TILES * TENS_PER_BANK
 
@@ -112,10 +115,7 @@ def unscramble(nc, z_grouped, z_rows, on_scalar):
         place, row = divmod(LEAD + CHANNELS * t + v, TOKENS)
         return row * ROW_PITCH + PAD + place
 
-    for v in range(TOKENS):
-        if (v in SCALAR_V) != on_scalar:
-            continue
-        engine_copy = nc.scalar.copy if on_scalar else nc.vector.tensor_copy
+    for v in some_v:
         at = [start_of(t, v) for t in range(PACK)]
         columns = banks[:, :, TENS_PER_BANK * v : TENS_PER_BANK * (v + 1), :]
         if at[1] - at[0] == at[3] - at[2]:
@@ -140,7 +140,7 @@ def unscramble(nc, z_grouped, z_rows, on_scalar):
                     out=columns[:, :, :, first : last + 1 : last - first],
                     in_=runs[:, :, 0:tens].rearrange("p e (n u) -> p n u e", n=N_TILES),
                 )
-    for h in range(0 if on_scalar else 2):
+    for h in range(2 if last_columns else 0):
         first = start_of(2 * h, 0) + tens
         far = start_of(2 * h + 1, 0) - start_of(2 * h, 0)
         assert far >= PACK * ROW_PITCH and first + 2 * far <= ROWS_ROOM
@@ -149,7 +149,7 @@ def unscramble(nc, z_grouped, z_rows, on_scalar):
             assert start_of(2 * h + 1, y) == start_of(2 * h + 1, 0) + y * ROW_PITCH
         runs = z_rows[:, first : first + 2 * far].rearrange("p (l s) -> p l s", l=2)
         runs = runs[:, :, 0 : 4 * ROW_PITCH].rearrange("p l (y q) -> p l y q", y=4)
-        nc.vector.tensor_copy(
+        engine_copy(
             out=banks[:, :, BANK_MAIN:N_TILE, 2 * h : 2 * h + 2],
             in_=runs[:, :, :, 0:1].rearrange("p l (n x) o -> p n x (l o)", n=N_TILES),
         )
@@ -199,11 +199,13 @@ def tile_attention_pa_kernel(tc, y_attn, w_proj, b_proj, grad_out, out):
             return z_stage.tile([P, CHANNELS, PACK], BF16, align_bytes=64, name="z_grouped")
 
         def quantise_z(z_grouped, blk):
-            nc.vector.quantize_mx(
-                out=z_codes[:, blk, :].bitcast(E4M3_X4),
-                scales=z_scales[:, blk, :],
-                in_=z_grouped[:].rearrange("p c t -> p (c t)"),
-            )
+            for n in range(N_TILES):
+                cols = slice(N_TILE * n, N_TILE * (n + 1))
+                nc.vector.quantize_mx(
+                    out=z_codes[:, blk, cols].bitcast(E4M3_X4),
+                    scales=z_scales[:, blk, cols],
+                    in_=z_grouped[:, cols, :].rearrange("p c t -> p (c t)"),
+                )
 
         def mx_pass(acc, blk, m, n):
             m_cols = slice(M_TILE * m, M_TILE * (m + 1))
@@ -221,8 +223,7 @@ def tile_attention_pa_kernel(tc, y_attn, w_proj, b_proj, grad_out, out):
         def new_row_out():
             return result.tile([P, CHANNELS], F32, name="row_out")
 
-        def empty_bank(row_out, acc, n):
-            engine_copy = (nc.vector.tensor_copy, nc.scalar.copy)[n]
+        def empty_bank(engine_copy, row_out, acc, n):
             engine_copy(
                 out=row_out[:, BANK_MAIN * n : BANK_MAIN * (n + 1)].rearrange("p (u v) -> p u v", v=TOKENS),
                 in_=acc[:, 0:BANK_MAIN].rearrange("p (v u) -> p u v", v=TOKENS),
@@ -241,7 +242,10 @@ def tile_attention_pa_kernel(tc, y_attn, w_proj, b_proj, grad_out, out):
 
         ctx.enter_context(tc.manual_schedule())
 
-        accs = [new_accs(m) for m in range(M_TILES_PER_HALF)]
+        accs = [[None] * N_TILES for m in range(M_TILES_PER_HALF)]
+        for n in range(N_TILES):
+            for m in range(M_TILES_PER_HALF):
+                accs[m][n] = psum.tile([P, N_TILE], F32, name="acc_%d_%d" % (m, n), tag="acc")
         nc.vector.memset(warm[:, 0:1], 0.0)
         nc.scalar.copy(out=warm[:, 1:2], in_=warm[:, 0:1])
         load_z_rows(nc, y_attn, y_groups, z_rows[0], first_pair, 0)
@@ -255,24 +259,53 @@ def tile_attention_pa_kernel(tc, y_attn, w_proj, b_proj, grad_out, out):
         for blk in range(PASSES):
             load_g(blk, 1)
 
-        for blk in range(PASSES):
-            z_grouped = new_z_grouped()
-            unscramble(nc, z_grouped[:], z_rows[blk], True)
-            g_grouped = regroup_g(blk, 0)
-            unscramble(nc, z_grouped[:], z_rows[blk], False)
-            quantise_g(g_grouped, blk, 0)
-            quantise_z(z_grouped, blk)
-            for m in range(M_TILES_PER_HALF):
-                for n in range(N_TILES):
+        def round_0(blk):
+            for n in range(N_TILES):
+                for m in range(M_TILES_PER_HALF):
                     mx_pass(accs[m][n], blk, m, n)
 
-        rows_out = [new_row_out() for m in range(M_TILES_PER_HALF)]
+        v_copy, s_copy = nc.vector.tensor_copy, nc.scalar.copy
+        g_grouped = [None] * PASSES
         for blk in range(PASSES):
-            quantise_g(regroup_g(blk, 1), blk, 1)
-            if blk < M_TILES_PER_HALF:
-                for n in range(N_TILES):
-                    empty_bank(rows_out[blk], accs[blk][n], n)
-                store_row(blk, rows_out[blk])
+            z_grouped = new_z_grouped()
+            unscramble(nc, z_grouped[:], z_rows[blk], s_copy, SCALAR_V, False)
+            g_grouped[blk] = regroup_g(blk, 0)
+            unscramble(nc, z_grouped[:], z_rows[blk], v_copy, VECTOR_V[0:1], False)
+            if blk > 0:
+                quantise_g(g_grouped[blk - 1], blk - 1, 0)
+                round_0(blk - 1)
+            unscramble(nc, z_grouped[:], z_rows[blk], v_copy, VECTOR_V[1:], True)
+            if blk == PASSES - 1:
+                quantise_g(g_grouped[blk], blk, 0)
+            quantise_z(z_grouped, blk)
+        round_0(PASSES - 1)
+
+        rows_out = [new_row_out() for m in range(M_TILES_PER_HALF)]
+        right = [None] * PASSES
+
+        def empty_0(engine_copy, m, n):
+            empty_bank(engine_copy, rows_out[m], accs[m][n], n)
+            if n == N_TILES - 1:
+                store_row(m, rows_out[m])
+
+        right[0] = regroup_g(0, 1)
+        right[1] = regroup_g(1, 1)
+        quantise_g(right[0], 0, 1)
+        empty_0(v_copy, 0, 0)
+        empty_0(s_copy, 1, 0)
+        empty_0(v_copy, 2, 0)
+        right[2] = regroup_g(2, 1)
+        empty_0(s_copy, 3, 0)
+        quantise_g(right[1], 1, 1)
+        quantise_g(right[2], 2, 1)
+        right[3] = regroup_g(3, 1)
+        right[4] = regroup_g(4, 1)
+        empty_0(v_copy, 0, 1)
+        quantise_g(right[3], 3, 1)
+        empty_0(v_copy, 1, 1)
+        quantise_g(right[4], 4, 1)
+        empty_0(v_copy, 2, 1)
+        empty_0(v_copy, 3, 1)
 
         first = [new_accs(m) for m in (4, 5)]
         for blk in range(PASSES):
@@ -287,10 +320,10 @@ def tile_attention_pa_kernel(tc, y_attn, w_proj, b_proj, grad_out, out):
             if m == 6:
                 for i in range(2):
                     row_out = new_row_out()
-                    for n in range(N_TILES):
-                        empty_bank(row_out, first[i][n], n)
+                    for n, engine_copy in enumerate((v_copy, s_copy)):
+                        empty_bank(engine_copy, row_out, first[i][n], n)
                     store_row(4 + i, row_out)
             row_out = new_row_out()
-            for n in range(N_TILES):
-                empty_bank(row_out, accs_m[n], n)
+            for n, engine_copy in enumerate((v_copy, s_copy)):
+                empty_bank(engine_copy, row_out, accs_m[n], n)
             store_row(m, row_out)

@@ -94,6 +94,10 @@ def load_z_rows(nc, y_attn, y_groups, z_rows, first_pair, blk):
                 place += count
 
 
+def regroup_in_turn(engine_copy, grouped, planes):
+    engine_copy(out=grouped, in_=planes.rearrange("p t c -> p c t"))
+
+
 def regroup(engine_copy, grouped, planes):
     engine_copy(
         out=grouped.rearrange("p (c i) t -> p c t i", i=4),
@@ -164,7 +168,7 @@ def tile_attention_pa_kernel(tc, y_attn, w_proj, b_proj, grad_out, out):
         keep = ctx.enter_context(tc.tile_pool(name="keep", bufs=1))
         z_stage = ctx.enter_context(tc.tile_pool(name="z_stage", bufs=2))
         g_stage = ctx.enter_context(tc.tile_pool(name="g_stage", bufs=6))
-        result = ctx.enter_context(tc.tile_pool(name="result", bufs=4))
+        result = ctx.enter_context(tc.tile_pool(name="result", bufs=6))
         psum = ctx.enter_context(tc.psum_pool(name="psum", bufs=8))
 
         z_rows = [keep.tile([P, ROWS_ROOM], BF16, name="z_rows_%d" % blk) for blk in range(PASSES)]
@@ -176,15 +180,18 @@ def tile_attention_pa_kernel(tc, y_attn, w_proj, b_proj, grad_out, out):
         g_codes = keep.tile([P, PASSES, FEATURES], U32, align_bytes=64)
         g_scales = keep.tile([P, PASSES, FEATURES], U8, align_bytes=64)
 
+        v_copy, s_copy = nc.vector.tensor_copy, nc.scalar.copy
+
         def load_g(blk, half):
             nc.sync.dma_start(
                 out=g_planes[:, blk, half],
                 in_=g_groups[:, BLOCK_ROWS * blk : BLOCK_ROWS * (blk + 1), HALF * half : HALF * (half + 1)],
             )
 
-        def regroup_g(blk, half):
+        def regroup_g(blk, half, engine_copy):
             g_grouped = g_stage.tile([P, HALF, PACK], BF16, align_bytes=64)
-            regroup(nc.scalar.copy, g_grouped[:], g_planes[:, blk, half])
+            in_order = regroup_in_turn if engine_copy is v_copy else regroup
+            in_order(engine_copy, g_grouped[:], g_planes[:, blk, half])
             return g_grouped
 
         def quantise_g(g_grouped, blk, half):
@@ -248,28 +255,26 @@ def tile_attention_pa_kernel(tc, y_attn, w_proj, b_proj, grad_out, out):
                 accs[m][n] = psum.tile([P, N_TILE], F32, name="acc_%d_%d" % (m, n), tag="acc")
         nc.vector.memset(warm[:, 0:1], 0.0)
         nc.scalar.copy(out=warm[:, 1:2], in_=warm[:, 0:1])
-        load_z_rows(nc, y_attn, y_groups, z_rows[0], first_pair, 0)
+        for blk in range(PASSES):
+            load_z_rows(nc, y_attn, y_groups, z_rows[blk], first_pair, blk)
+            load_g(blk, 0)
+        for blk in range(PASSES):
+            load_g(blk, 1)
         nc.vector.tensor_copy(
             out=z_rows[0][0:1, LEAD * ROW_PITCH + PAD : LEAD * ROW_PITCH + PAD + 2], in_=first_pair[0:1, :]
         )
-        for blk in range(PASSES):
-            load_g(blk, 0)
-            if blk + 1 < PASSES:
-                load_z_rows(nc, y_attn, y_groups, z_rows[blk + 1], first_pair, blk + 1)
-        for blk in range(PASSES):
-            load_g(blk, 1)
 
         def round_0(blk):
             for n in range(N_TILES):
                 for m in range(M_TILES_PER_HALF):
                     mx_pass(accs[m][n], blk, m, n)
 
-        v_copy, s_copy = nc.vector.tensor_copy, nc.scalar.copy
         g_grouped = [None] * PASSES
+        right = [None] * PASSES
         for blk in range(PASSES):
             z_grouped = new_z_grouped()
             unscramble(nc, z_grouped[:], z_rows[blk], s_copy, SCALAR_V, False)
-            g_grouped[blk] = regroup_g(blk, 0)
+            g_grouped[blk] = regroup_g(blk, 0, s_copy)
             unscramble(nc, z_grouped[:], z_rows[blk], v_copy, VECTOR_V[0:1], False)
             if blk > 0:
                 quantise_g(g_grouped[blk - 1], blk - 1, 0)
@@ -281,30 +286,29 @@ def tile_attention_pa_kernel(tc, y_attn, w_proj, b_proj, grad_out, out):
         round_0(PASSES - 1)
 
         rows_out = [new_row_out() for m in range(M_TILES_PER_HALF)]
-        right = [None] * PASSES
 
         def empty_0(engine_copy, m, n):
             empty_bank(engine_copy, rows_out[m], accs[m][n], n)
             if n == N_TILES - 1:
                 store_row(m, rows_out[m])
 
-        right[0] = regroup_g(0, 1)
-        right[1] = regroup_g(1, 1)
+        right[0] = regroup_g(0, 1, s_copy)
+        right[1] = regroup_g(1, 1, s_copy)
         quantise_g(right[0], 0, 1)
         empty_0(v_copy, 0, 0)
         empty_0(s_copy, 1, 0)
         empty_0(v_copy, 2, 0)
-        right[2] = regroup_g(2, 1)
-        empty_0(s_copy, 3, 0)
+        right[2] = regroup_g(2, 1, s_copy)
+        empty_0(v_copy, 3, 0)
         quantise_g(right[1], 1, 1)
+        right[3] = regroup_g(3, 1, v_copy)
         quantise_g(right[2], 2, 1)
-        right[3] = regroup_g(3, 1)
-        right[4] = regroup_g(4, 1)
-        empty_0(v_copy, 0, 1)
         quantise_g(right[3], 3, 1)
-        empty_0(v_copy, 1, 1)
+        right[4] = regroup_g(4, 1, s_copy)
+        empty_0(v_copy, 0, 1)
         quantise_g(right[4], 4, 1)
-        empty_0(v_copy, 2, 1)
+        empty_0(v_copy, 1, 1)
+        empty_0(s_copy, 2, 1)
         empty_0(v_copy, 3, 1)
 
         first = [new_accs(m) for m in (4, 5)]

@@ -29,7 +29,8 @@ LEAD = 2
 RUN = (LEAD + WORD_ELEMS + TOKENS - 1) // TOKENS
 RUN_COLUMNS = TOKENS * ((CHANNELS + TOKENS - 1) // TOKENS)
 PAD = 3
-ROW_PITCH = 416
+ROW_LOADED = 416
+ROW_PITCH = 512
 ROWS_ROOM = 14 * ROW_PITCH
 
 M_TILE = 128
@@ -79,7 +80,7 @@ def load_z_rows(nc, y_attn, y_groups, z_rows, first_pair, blk):
             place = 1 if row_hi <= LEAD else 0
             last_place = RUN - 2 if row_lo >= TOKENS - LEAD else RUN - 1
             place -= min(PAD + place, (first_channel + carry + place) % CHANNELS)
-            last_place += min(ROW_PITCH - 1 - PAD - last_place, CHANNELS - 1 - (first_channel + carry + last_place) % CHANNELS)
+            last_place += min(ROW_LOADED - 1 - PAD - last_place, CHANNELS - 1 - (first_channel + carry + last_place) % CHANNELS)
             while place <= last_place:
                 image, channel = divmod(first_channel + carry + place, CHANNELS)
                 count = min(last_place - place + 1, CHANNELS - channel)
@@ -171,10 +172,10 @@ def tile_attention_pa_kernel(tc, y_attn, w_proj, b_proj, grad_out, out):
         result = ctx.enter_context(tc.tile_pool(name="result", bufs=6))
         psum = ctx.enter_context(tc.psum_pool(name="psum", bufs=8))
 
-        z_rows = [keep.tile([P, ROWS_ROOM], BF16, name="z_rows_%d" % blk) for blk in range(PASSES)]
+        z_rows = [keep.tile([P, ROWS_ROOM], BF16, align_bytes=256, name="z_rows_%d" % blk) for blk in range(PASSES)]
         first_pair = keep.tile([P, 2], BF16)
         warm = keep.tile([P, 2], F32)
-        g_planes = keep.tile([P, PASSES, 2, PACK, HALF], BF16)
+        g_planes = keep.tile([P, PASSES, 2, PACK, HALF], BF16, align_bytes=256)
         z_codes = keep.tile([P, PASSES, CHANNELS], U32, align_bytes=64)
         z_scales = keep.tile([P, PASSES, CHANNELS], U8, align_bytes=64)
         g_codes = keep.tile([P, PASSES, FEATURES], U32, align_bytes=64)
@@ -228,7 +229,7 @@ def tile_attention_pa_kernel(tc, y_attn, w_proj, b_proj, grad_out, out):
             )
 
         def new_row_out():
-            return result.tile([P, CHANNELS], F32, name="row_out")
+            return result.tile([P, CHANNELS], F32, align_bytes=256, name="row_out")
 
         def empty_bank(engine_copy, row_out, acc, n):
             engine_copy(

from contextlib import ExitStack

import concourse.mybir as mybir

FLOPS = 2 * 2560 * 1024 * 1024
BYTES = 2 * 2560 * 1024 * 2 + 1024 * 1024 * 4

BF16 = mybir.dt.bfloat16
F32 = mybir.dt.float32
U32 = mybir.dt.uint32
U8 = mybir.dt.uint8
E4M3_X4 = mybir.dt.float8_e4m3fn_x4
E5M2_X4 = mybir.dt.float8_e5m2_x4

P = 128
PACK = 4
TOKENS = 10
CHANNELS = 1024
FEATURES = 1024
BLOCK_ROWS = 32
BLOCK_PARTS = BLOCK_ROWS // PACK
GROUP_IMAGES = 16
GROUP_ROWS = GROUP_IMAGES * TOKENS
GROUPS = P // BLOCK_PARTS
PASSES = GROUP_ROWS // BLOCK_ROWS

WORD_ELEMS = PACK * CHANNELS
LEAD = 2
RUN = (LEAD + WORD_ELEMS + TOKENS - 1) // TOKENS
RUN_COLUMNS = TOKENS * ((CHANNELS + TOKENS - 1) // TOKENS)
PAD = 3
ROW_LOADED = 416
ROW_PITCH = 512
ROWS_ROOM = 14 * ROW_PITCH

M_TILE = 128
N_TILE = 512
HALF = FEATURES // 2
M_TILES_PER_HALF = HALF // M_TILE
N_TILES = CHANNELS // N_TILE
TENS_PER_BANK = N_TILE // TOKENS
BANK_MAIN = TOKENS * TENS_PER_BANK


def load_from_one_before(nc, queue, y_attn, rows, first_pair, w, row_lo, row_hi, at, image, token_lo, channel, count):
    assert channel == 0
    y_stream = y_attn.rearrange("b tok c -> (b tok c)")
    y_flat = y_attn.rearrange("(grp img) tok c -> grp (img tok c)", img=GROUP_IMAGES)
    skip = 1 if image == 0 and token_lo == 0 else 0
    rows_left = row_hi - row_lo - skip
    start = (image * TOKENS + token_lo + skip) * CHANNELS - 1
    queue.dma_start(
        out=rows[w:P:BLOCK_PARTS, row_lo + skip : row_hi, at - 1 : at + count],
        in_=y_flat[:, start : start + rows_left * CHANNELS].rearrange("g (t c) -> g t c", c=CHANNELS)[:, :, 0 : count + 1],
    )
    if skip:
        group_elems = GROUP_IMAGES * TOKENS * CHANNELS
        later_groups = y_stream[group_elems - 1 : GROUPS * group_elems - 1].rearrange("(g x) -> g x", x=group_elems)
        queue.dma_start(
            out=rows[w + BLOCK_PARTS : P : BLOCK_PARTS, row_lo, at - 1 : at + count],
            in_=later_groups[:, 0 : count + 1],
        )
        queue.dma_start(out=rows[w : w + 1, row_lo, at + 1 : at + count], in_=y_attn[0:1, 0, 1:count])
        queue.dma_start(out=first_pair[0:1, :], in_=y_attn[0:1, 0, 0:2])


def load_z_rows(nc, y_attn, y_groups, z_rows, first_pair, blk):
    rows = z_rows[:, 0 : TOKENS * ROW_PITCH].rearrange("p (r q) -> p r q", q=ROW_PITCH)
    for i in range(BLOCK_PARTS):
        w = (i % 2) * (BLOCK_PARTS // 2) + i // 2
        queue = nc.sync
        window_start = WORD_ELEMS * (BLOCK_PARTS * blk + w) - LEAD
        first_channel, first_token = divmod(window_start, TOKENS)
        turn = TOKENS - first_token
        for row_lo, row_hi, carry in ((0, turn, 0), (turn, TOKENS, 1)):
            if row_lo == row_hi:
                continue
            token_lo = first_token + row_lo - TOKENS * carry
            token_hi = token_lo + row_hi - row_lo
            place = 1 if row_hi <= LEAD else 0
            last_place = RUN - 2 if row_lo >= TOKENS - LEAD else RUN - 1
            place -= min(PAD + place, (first_channel + carry + place) % CHANNELS)
            last_place += min(ROW_LOADED - 1 - PAD - last_place, CHANNELS - 1 - (first_channel + carry + last_place) % CHANNELS)
            while place <= last_place:
                image, channel = divmod(first_channel + carry + place, CHANNELS)
                count = min(last_place - place + 1, CHANNELS - channel)
                at = PAD + place
                if at % 2 == 0:
                    queue.dma_start(
                        out=rows[w:P:BLOCK_PARTS, row_lo:row_hi, at : at + count],
                        in_=y_groups[:, image, token_lo:token_hi, channel : channel + count],
                    )
                else:
                    load_from_one_before(nc, queue, y_attn, rows, first_pair, w, row_lo, row_hi, at, image, token_lo, channel, count)
                place += count


def regroup_in_turn(engine_copy, grouped, planes):
    engine_copy(out=grouped, in_=planes.rearrange("p t c -> p c t"))


def regroup(engine_copy, grouped, planes):
    engine_copy(
        out=grouped.rearrange("p (c i) t -> p c t i", i=4),
        in_=planes.rearrange("p t (c i) -> p c t i", i=4),
    )


SCALAR_V = (6, 7)


VECTOR_V = tuple(v for v in range(TOKENS) if v not in SCALAR_V)


def unscramble(nc, z_grouped, z_rows, engine_copy, some_v, last_columns):
    banks = z_grouped.rearrange("p (n c) t -> p n c t", n=N_TILES)
    tens = N_TILES * TENS_PER_BANK

    def start_of(t, v):
        place, row = divmod(LEAD + CHANNELS * t + v, TOKENS)
        return row * ROW_PITCH + PAD + place

    for v in some_v:
        at = [start_of(t, v) for t in range(PACK)]
        columns = banks[:, :, TENS_PER_BANK * v : TENS_PER_BANK * (v + 1), :]
        if at[1] - at[0] == at[3] - at[2]:
            far, near = at[1] - at[0], at[2] - at[0]
            assert abs(far) >= 2 * abs(near) and abs(near) >= tens and min(at) + 2 * abs(far) <= ROWS_ROOM
            runs = z_rows[:, min(at) : min(at) + 2 * abs(far)].rearrange("p (l s) -> p l s", l=2)
            runs = runs[:, :, 0 : 2 * abs(near)].rearrange("p l (h s) -> p l h s", h=2)
            if far < 0:
                runs = runs[:, ::-1]
            if near < 0:
                runs = runs[:, :, ::-1]
            engine_copy(
                out=columns.rearrange("p n u (h l) -> p n u h l", h=2),
                in_=runs[:, :, :, 0:tens].rearrange("p l h (n u) -> p n u h l", n=N_TILES),
            )
        else:
            for first, last in ((0, 3), (1, 2)):
                apart = at[last] - at[first]
                assert apart >= tens and at[first] + 2 * apart <= ROWS_ROOM
                runs = z_rows[:, at[first] : at[first] + 2 * apart].rearrange("p (e s) -> p e s", e=2)
                engine_copy(
                    out=columns[:, :, :, first : last + 1 : last - first],
                    in_=runs[:, :, 0:tens].rearrange("p e (n u) -> p n u e", n=N_TILES),
                )
    for h in range(2 if last_columns else 0):
        first = start_of(2 * h, 0) + tens
        far = start_of(2 * h + 1, 0) - start_of(2 * h, 0)
        assert far >= PACK * ROW_PITCH and first + 2 * far <= ROWS_ROOM
        for y in range(1, 4):
            assert start_of(2 * h, y) == start_of(2 * h, 0) + y * ROW_PITCH
            assert start_of(2 * h + 1, y) == start_of(2 * h + 1, 0) + y * ROW_PITCH
        runs = z_rows[:, first : first + 2 * far].rearrange("p (l s) -> p l s", l=2)
        runs = runs[:, :, 0 : 4 * ROW_PITCH].rearrange("p l (y q) -> p l y q", y=4)
        engine_copy(
            out=banks[:, :, BANK_MAIN:N_TILE, 2 * h : 2 * h + 2],
            in_=runs[:, :, :, 0:1].rearrange("p l (n x) o -> p n x (l o)", n=N_TILES),
        )


def tile_attention_pa_kernel(tc, y_attn, w_proj, b_proj, grad_out, out):
    nc = tc.nc
    y_groups = y_attn.rearrange("(grp img) tok c -> grp img tok c", img=GROUP_IMAGES)
    g_groups = grad_out.rearrange("(grp img) i c -> grp (img i) c", img=GROUP_IMAGES)

    with ExitStack() as ctx:
        keep = ctx.enter_context(tc.tile_pool(name="keep", bufs=1))
        z_stage = ctx.enter_context(tc.tile_pool(name="z_stage", bufs=2))
        g_stage = ctx.enter_context(tc.tile_pool(name="g_stage", bufs=6))
        result = ctx.enter_context(tc.tile_pool(name="result", bufs=6))
        psum = ctx.enter_context(tc.psum_pool(name="psum", bufs=8))

        z_rows = [keep.tile([P, ROWS_ROOM], BF16, align_bytes=256, name="z_rows_%d" % blk) for blk in range(PASSES)]
        first_pair = keep.tile([P, 2], BF16)
        warm = keep.tile([P, 2], F32)
        g_planes = keep.tile([P, PASSES, 2, PACK, HALF], BF16, align_bytes=256)
        z_codes = keep.tile([P, PASSES, CHANNELS], U32, align_bytes=64)
        z_scales = keep.tile([P, PASSES, CHANNELS], U8, align_bytes=64)
        g_codes = keep.tile([P, PASSES, FEATURES], U32, align_bytes=64)
        g_scales = keep.tile([P, PASSES, FEATURES], U8, align_bytes=64)

        v_copy, s_copy = nc.vector.tensor_copy, nc.scalar.copy

        def load_g(blk, half):
            nc.sync.dma_start(
                out=g_planes[:, blk, half],
                in_=g_groups[:, BLOCK_ROWS * blk : BLOCK_ROWS * (blk + 1), HALF * half : HALF * (half + 1)],
            )

        def regroup_g(blk, half, engine_copy):
            g_grouped = g_stage.tile([P, HALF, PACK], BF16, align_bytes=64)
            in_order = regroup_in_turn if engine_copy is v_copy else regroup
            in_order(engine_copy, g_grouped[:], g_planes[:, blk, half])
            return g_grouped

        def quantise_g(g_grouped, blk, half):
            cols = slice(HALF * half, HALF * (half + 1))
            nc.vector.quantize_mx(
                out=g_codes[:, blk, cols].bitcast(E5M2_X4),
                scales=g_scales[:, blk, cols],
                in_=g_grouped[:].rearrange("p c t -> p (c t)"),
            )

        def new_z_grouped():
            return z_stage.tile([P, CHANNELS, PACK], BF16, align_bytes=64, name="z_grouped")

        def quantise_z(z_grouped, blk):
            for n in range(N_TILES):
                cols = slice(N_TILE * n, N_TILE * (n + 1))
                nc.vector.quantize_mx(
                    out=z_codes[:, blk, cols].bitcast(E4M3_X4),
                    scales=z_scales[:, blk, cols],
                    in_=z_grouped[:, cols, :].rearrange("p c t -> p (c t)"),
                )

        def mx_pass(acc, blk, m, n):
            m_cols = slice(M_TILE * m, M_TILE * (m + 1))
            n_cols = slice(N_TILE * n, N_TILE * (n + 1))
            nc.tensor.matmul_mx(
                out=acc[:],
                lhsT=g_codes[:, blk, m_cols].bitcast(E5M2_X4),
                lhsT_scale=g_scales[:, blk, m_cols],
                rhs=z_codes[:, blk, n_cols].bitcast(E4M3_X4),
                rhs_scale=z_scales[:, blk, n_cols],
                start=(blk == 0),
                stop=(blk == PASSES - 1),
            )

        def new_row_out():
            return result.tile([P, CHANNELS], F32, align_bytes=256, name="row_out")

        def empty_bank(engine_copy, row_out, acc, n):
            engine_copy(
                out=row_out[:, BANK_MAIN * n : BANK_MAIN * (n + 1)].rearrange("p (u v) -> p u v", v=TOKENS),
                in_=acc[:, 0:BANK_MAIN].rearrange("p (v u) -> p u v", v=TOKENS),
            )
            rest = N_TILE - BANK_MAIN
            engine_copy(
                out=row_out[:, N_TILES * BANK_MAIN + rest * n : N_TILES * BANK_MAIN + rest * (n + 1)],
                in_=acc[:, BANK_MAIN:N_TILE],
            )

        def store_row(m, row_out):
            nc.sync.dma_start(out=out[M_TILE * m : M_TILE * (m + 1), :], in_=row_out[:])

        def new_accs(m):
            return [psum.tile([P, N_TILE], F32, name="acc_%d_%d" % (m, n), tag="acc") for n in range(N_TILES)]

        ctx.enter_context(tc.manual_schedule())

        accs = [[None] * N_TILES for m in range(M_TILES_PER_HALF)]
        for n in range(N_TILES):
            for m in range(M_TILES_PER_HALF):
                accs[m][n] = psum.tile([P, N_TILE], F32, name="acc_%d_%d" % (m, n), tag="acc")
        nc.vector.memset(warm[:, 0:1], 0.0)
        nc.scalar.copy(out=warm[:, 1:2], in_=warm[:, 0:1])
        for blk in range(PASSES):
            load_z_rows(nc, y_attn, y_groups, z_rows[blk], first_pair, blk)
            load_g(blk, 0)
        for blk in range(PASSES):
            load_g(blk, 1)
        nc.vector.tensor_copy(
            out=z_rows[0][0:1, LEAD * ROW_PITCH + PAD : LEAD * ROW_PITCH + PAD + 2], in_=first_pair[0:1, :]
        )

        def round_0(blk):
            for n in range(N_TILES):
                for m in range(M_TILES_PER_HALF):
                    mx_pass(accs[m][n], blk, m, n)

        g_grouped = [None] * PASSES
        right = [None] * PASSES
        for blk in range(PASSES):
            z_grouped = new_z_grouped()
            unscramble(nc, z_grouped[:], z_rows[blk], s_copy, SCALAR_V, False)
            g_grouped[blk] = regroup_g(blk, 0, s_copy)
            unscramble(nc, z_grouped[:], z_rows[blk], v_copy, VECTOR_V[0:1], False)
            if blk > 0:
                quantise_g(g_grouped[blk - 1], blk - 1, 0)
                round_0(blk - 1)
            unscramble(nc, z_grouped[:], z_rows[blk], v_copy, VECTOR_V[1:], True)
            if blk == PASSES - 1:
                quantise_g(g_grouped[blk], blk, 0)
            quantise_z(z_grouped, blk)
        round_0(PASSES - 1)

        rows_out = [new_row_out() for m in range(M_TILES_PER_HALF)]

        def empty_0(engine_copy, m, n):
            empty_bank(engine_copy, rows_out[m], accs[m][n], n)
            if n == N_TILES - 1:
                store_row(m, rows_out[m])

        right[0] = regroup_g(0, 1, s_copy)
        right[1] = regroup_g(1, 1, s_copy)
        quantise_g(right[0], 0, 1)
        empty_0(v_copy, 0, 0)
        empty_0(s_copy, 1, 0)
        empty_0(v_copy, 2, 0)
        right[2] = regroup_g(2, 1, s_copy)
        empty_0(v_copy, 3, 0)
        quantise_g(right[1], 1, 1)
        right[3] = regroup_g(3, 1, v_copy)
        quantise_g(right[2], 2, 1)
        quantise_g(right[3], 3, 1)
        right[4] = regroup_g(4, 1, s_copy)
        empty_0(v_copy, 0, 1)
        quantise_g(right[4], 4, 1)
        empty_0(v_copy, 1, 1)
        empty_0(s_copy, 2, 1)
        empty_0(v_copy, 3, 1)

        first = [new_accs(m) for m in (4, 5)]
        for blk in range(PASSES):
            for i in range(2):
                for n in range(N_TILES):
                    mx_pass(first[i][n], blk, 4 + i, n)
        for m in (6, 7):
            accs_m = new_accs(m)
            for n in range(N_TILES):
                for blk in range(PASSES):
                    mx_pass(accs_m[n], blk, m, n)
            if m == 6:
                for i in range(2):
                    row_out = new_row_out()
                    for n, engine_copy in enumerate((v_copy, s_copy)):
                        empty_bank(engine_copy, row_out, first[i][n], n)
                    store_row(4 + i, row_out)
            row_out = new_row_out()
            for n, engine_copy in enumerate((v_copy, s_copy)):
                empty_bank(engine_copy, row_out, accs_m[n], n)
            store_row(m, row_out)
